import numpy as np
import ml_dtypes


def mxq(x, axis, fmt="e4m3"):
    dtype, down = {"e4m3": (ml_dtypes.float8_e4m3fn, 7), "e5m2": (ml_dtypes.float8_e5m2, 14)}[fmt]
    v = np.moveaxis(np.asarray(x, np.float32).astype(ml_dtypes.bfloat16).astype(np.float64), axis, -1)
    blocks = v.reshape(v.shape[:-1] + (-1, 32))
    amax = np.abs(blocks).max(-1, keepdims=True)
    byte = np.maximum(np.where(amax > 0, np.frexp(amax)[1] - 1 + 127, 0) - down, 1)
    scale = np.exp2(byte - 127.0)
    codes = (blocks / scale).astype(np.float32).astype(dtype).astype(np.float64)
    return np.moveaxis((codes * scale).reshape(v.shape), -1, axis)


WIDE = False


def mx_kscale(k):
    if not WIDE:
        return np.ones(k)
    levels = np.array([10, -10, 5, -5, 0])
    a = np.random.permutation(np.resize(levels, k // 512 * 4)).reshape(k // 512, 4)
    idx = np.arange(k)
    return np.exp2(a[idx // 512, idx % 128 // 32])


BF16 = ml_dtypes.bfloat16


def bf(x):
    return np.asarray(x, np.float32).astype(BF16)


def f64(x):
    return np.asarray(x).astype(np.float64)


B, N, E, H, NOPE, VDIM, ROPE, QR, KVR = 4, 1024, 1024, 4, 64, 64, 128, 512, 512
KVH = NOPE + VDIM
BASE = 10000.0


def rope(v):
    d = v.shape[-1]
    n = v.shape[-2]
    theta = BASE ** (-2.0 * np.arange(d // 2) / d)
    ang = np.arange(n)[:, None] * theta[None, :]
    cos, sin = np.cos(ang), np.sin(ang)
    v1, v2 = v[..., 0::2], v[..., 1::2]
    return np.stack([v1 * cos - v2 * sin, v1 * sin + v2 * cos], axis=-1).reshape(v.shape)


def setup_inputs():
    s, t = mx_kscale(E), mx_kscale(KVR)
    tcol = np.concatenate([t, np.ones(ROPE)])
    return {"x": bf(np.random.standard_normal((B, N, E)) * s),
            "Wkva": bf(np.random.standard_normal((E, KVR + ROPE)) / np.sqrt(E) / s[:, None] * tcol),
            "Wkvb": bf(np.random.standard_normal((KVR, H * KVH)) / np.sqrt(KVR) / t[:, None])}


def reference(x, Wkva, Wkvb):
    ckv = mxq(f64(x), 2, "e4m3") @ mxq(f64(Wkva), 0, "e4m3")
    compressed, k_pe = ckv[..., :KVR], ckv[..., KVR:]
    k_pe = np.broadcast_to(k_pe[:, None], (B, H, N, ROPE))
    kv = mxq(compressed, 2, "e4m3") @ mxq(f64(Wkvb), 0, "e4m3")
    kv = kv.reshape(B, N, H, KVH).transpose(0, 2, 1, 3)
    k_nope, v = kv[..., :NOPE], kv[..., NOPE:]
    kf = np.concatenate([k_nope, rope(k_pe)], axis=-1)
    return kf, v

@@ -1,0 +1,343 @@
+import math
+from contextlib import ExitStack
+
+import concourse.bass as bass
+import concourse.mybir as mybir
+import concourse.tile as tile
+from concourse.masks import make_identity
+
+F32 = mybir.dt.float32
+BF16 = mybir.dt.bfloat16
+U32 = mybir.dt.uint32
+U8 = mybir.dt.uint8
+I32 = mybir.dt.int32
+FP8X4 = mybir.dt.float8_e4m3fn_x4
+ALU = mybir.AluOpType
+ACT = mybir.ActivationFunctionType
+
+P = 128
+B, N, E, H, NOPE, VDIM, ROPE, KVR = 4, 1024, 1024, 4, 64, 64, 128, 512
+BASE = 10000.0
+WA = KVR + ROPE
+UNITS = 8
+FLOPS = 2 * B * N * E * WA + 2 * B * N * KVR * H * (NOPE + VDIM)
+MANUAL = True
+
+
+def tile_multilatentattention_pb_t_kernel(tc, x, Wkva, Wkvb, out_0, out_1):
+    nc = tc.nc
+    with ExitStack() as ctx:
+        if MANUAL:
+            ctx.enter_context(tc.manual_schedule())
+        const = ctx.enter_context(tc.tile_pool(name="const", bufs=1))
+        work = ctx.enter_context(tc.tile_pool(name="work", bufs=2))
+        outp = ctx.enter_context(tc.tile_pool(name="outp", bufs=3))
+        ps_xt = ctx.enter_context(tc.psum_pool(name="ps_xt", bufs=3))
+        ps_ct = ctx.enter_context(tc.psum_pool(name="ps_ct", bufs=2))
+        ps_kv = ctx.enter_context(tc.psum_pool(name="ps_kv", bufs=2))
+        ps_kp = ctx.enter_context(tc.psum_pool(name="ps_kp", bufs=1))
+
+        wa_raw = const.tile([P, 2, 4, WA], BF16)
+        for g in range(2):
+            nc.sync.dma_start(
+                out=wa_raw[:, g, :, :].rearrange("p (u e) c -> p u (e c)", e=2),
+                in_=Wkva[512 * g : 512 * (g + 1), :].rearrange("(u q e) c -> q u (e c)", u=2, e=2),
+            )
+        x_sb = []
+        for i in range(UNITS):
+            x_sb.append(const.tile([P, 4, E], BF16, name="x_sb%d" % i))
+        wb_raw = const.tile([P, 4, 512], BF16)
+
+        def load_x(i, t_lo, t_n):
+            src = x[i // 2].rearrange("(p t) k -> p t k", t=8)
+            t0 = 4 * (i % 2)
+            nc.sync.dma_start(out=x_sb[i][:, t_lo : t_lo + t_n, :], in_=src[:, t0 + t_lo : t0 + t_lo + t_n, :])
+
+        load_x(0, 0, 2)
+        load_x(0, 2, 2)
+        load_x(1, 0, 4)
+        nc.sync.dma_start(out=wb_raw[:], in_=Wkvb.rearrange("(t p) n -> p t n", p=P))
+        for i in range(2, UNITS):
+            load_x(i, 0, 4)
+
+        ident = const.tile([P, P], F32)
+        make_identity(nc, ident[:])
+        n_i = const.tile([P, 8], I32)
+        nc.gpsimd.iota(out=n_i[:], pattern=[[1, 8]], base=0, channel_multiplier=8)
+
+        ab = const.tile([P, 16], F32)
+        one = const.tile([P, 1], F32)
+        nc.vector.memset(one[:], 1.0)
+        for a in range(8):
+            nc.vector.tensor_scalar_mul(out=ab[:, a : a + 1], in0=one[:], scalar1=BASE ** (-2.0 * 8 * a / ROPE) / (2.0 * math.pi))
+        for b in range(8):
+            nc.vector.tensor_scalar_mul(out=ab[:, 8 + b : 9 + b], in0=one[:], scalar1=BASE ** (-2.0 * b / ROPE))
+        u_t = const.tile([P, 8, 8], F32)
+        nc.vector.tensor_tensor(
+            out=u_t[:],
+            in0=ab[:, 0:8].unsqueeze(2).to_broadcast([P, 8, 8]),
+            in1=ab[:, 8:16].unsqueeze(1).to_broadcast([P, 8, 8]),
+            op=ALU.mult,
+        )
+        n_f = const.tile([P, 8], F32)
+        nc.vector.tensor_copy(out=n_f[:], in_=n_i[:])
+        t_a = const.tile([P, 8, 64], F32)
+        t_b = const.tile([P, 8, 64], F32)
+        t_k = const.tile([P, 8, 64], I32)
+        nc.vector.tensor_tensor(
+            out=t_a[:],
+            in0=n_f[:].unsqueeze(2).to_broadcast([P, 8, 64]),
+            in1=u_t[:].rearrange("p a b -> p (a b)").unsqueeze(1).to_broadcast([P, 8, 64]),
+            op=ALU.mult,
+        )
+        nc.vector.tensor_copy(out=t_k[:], in_=t_a[:])
+        nc.vector.tensor_copy(out=t_b[:], in_=t_k[:])
+        nc.vector.tensor_tensor(out=t_a[:], in0=t_a[:], in1=t_b[:], op=ALU.subtract)
+        nc.vector.scalar_tensor_tensor(out=t_b[:], in0=t_a[:], scalar=0.5, in1=t_a[:], op0=ALU.is_gt, op1=ALU.subtract)
+        nc.vector.scalar_tensor_tensor(out=t_a[:], in0=t_b[:], scalar=-1.0, in1=t_b[:], op0=ALU.mult, op1=ALU.min)
+        nc.vector.tensor_scalar_add(out=t_a[:], in0=t_a[:], scalar1=0.25)
+        cs = const.tile([P, 8, 4, 64], F32)
+        nc.scalar.activation(out=cs[:, :, 0, :], in_=t_a[:], func=ACT.Sin, scale=2.0 * math.pi)
+        nc.scalar.activation(out=cs[:, :, 1, :], in_=t_b[:], func=ACT.Sin, scale=-2.0 * math.pi)
+        nc.scalar.activation(out=cs[:, :, 2, :], in_=t_b[:], func=ACT.Sin, scale=2.0 * math.pi)
+        nc.scalar.activation(out=cs[:, :, 3, :], in_=t_a[:], func=ACT.Sin, scale=2.0 * math.pi)
+
+        wa_g = const.tile([P, 2, WA, 4], BF16, align_bytes=64)
+        wa_c = const.tile([P, 2, WA], U32, align_bytes=64)
+        wa_s = const.tile([P, 2, WA], U8, align_bytes=64)
+        for g in range(2):
+            nc.vector.tensor_copy(
+                out=wa_g[:, g, 0:KVR, :].rearrange("p (c i) t -> p c t i", i=4),
+                in_=wa_raw[:, g, :, 0:KVR].rearrange("p t (c i) -> p c t i", i=4),
+            )
+            nc.scalar.copy(
+                out=wa_g[:, g, KVR:WA, :].rearrange("p (h i) t -> p h i t", h=2),
+                in_=wa_raw[:, g, :, KVR:WA].rearrange("p t (i h) -> p h i t", h=2),
+            )
+        for g in range(2):
+            nc.vector.quantize_mx(
+                out=wa_c[:, g, 0:KVR].bitcast(FP8X4),
+                scales=wa_s[:, g, 0:KVR],
+                in_=wa_g[:, g, 0:KVR, :].rearrange("p w t -> p (w t)"),
+            )
+
+        def quant_rope_w():
+            for g in range(2):
+                nc.vector.quantize_mx(
+                    out=wa_c[:, g, KVR:WA].bitcast(FP8X4),
+                    scales=wa_s[:, g, KVR:WA],
+                    in_=wa_g[:, g, KVR:WA, :].rearrange("p w t -> p (w t)"),
+                )
+
+        wb_g = const.tile([P, 512, 4], BF16, align_bytes=64)
+        wb_c = const.tile([P, 512], U32, align_bytes=64)
+        wb_s = const.tile([P, 512], U8, align_bytes=64)
+
+        def prep_wb():
+            nc.vector.tensor_copy(
+                out=wb_g[:].rearrange("p (c i) t -> p c t i", i=4),
+                in_=wb_raw[:].rearrange("p t (c i) -> p c t i", i=4),
+            )
+            nc.vector.quantize_mx(out=wb_c[:].bitcast(FP8X4), scales=wb_s[:], in_=wb_g[:].rearrange("p w t -> p (w t)"))
+
+        st = {}
+
+        def transposes(i, q):
+            pr, g = q // 2, q % 2
+            xt = ps_xt.tile([P, 2, 256], F32, name="xt")
+            for u in range(2):
+                for jj in range(2):
+                    c0 = 256 * g + 128 * u
+                    nc.tensor.transpose(
+                        xt[:, u, 128 * jj : 128 * (jj + 1)],
+                        x_sb[i][:, 2 * pr + jj, :].bitcast(F32)[:, c0 : c0 + 128],
+                        ident[:],
+                    )
+            st[("xt", i, q)] = xt
+            if q == 0:
+                st[("xg", i)] = work.tile([P, 2048], F32, name="xg", align_bytes=64)
+                st[("xc", i)] = work.tile([P, 1024], U32, name="xc", align_bytes=64)
+                st[("xs", i)] = work.tile([P, 1024], U8, name="xs", align_bytes=64)
+
+        def x_out(i, q, eng):
+            xg = st[("xg", i)]
+            dst = xg[:, 512 * q : 512 * (q + 1)].rearrange("p (r u) -> p r u", u=2)
+            src = st[("xt", i, q)][:].rearrange("p u r -> p r u")
+            if eng == "s":
+                nc.scalar.copy(out=dst, in_=src)
+            else:
+                nc.vector.tensor_copy(out=dst, in_=src)
+
+        def quant_x(i, pr):
+            nc.vector.quantize_mx(
+                out=st[("xc", i)][:, 512 * pr : 512 * (pr + 1)].bitcast(FP8X4),
+                scales=st[("xs", i)][:, 512 * pr : 512 * (pr + 1)],
+                in_=st[("xg", i)][:, 1024 * pr : 1024 * (pr + 1)].bitcast(BF16),
+            )
+
+        def x_cols(j, g):
+            c0 = ((j // 2) * 2 + g) * 256 + (j % 2) * 128
+            return slice(c0, c0 + 128)
+
+        def rope_mm(i):
+            kp = ps_kp.tile([P, 4, ROPE], F32, name="kp")
+            for j in range(4):
+                for g in range(2):
+                    nc.tensor.matmul_mx(
+                        out=kp[:, j, :],
+                        lhsT=st[("xc", i)][:, x_cols(j, g)].bitcast(FP8X4),
+                        lhsT_scale=st[("xs", i)][:, x_cols(j, g)],
+                        rhs=wa_c[:, g, KVR:WA].bitcast(FP8X4),
+                        rhs_scale=wa_s[:, g, KVR:WA],
+                        start=(g == 0),
+                        stop=(g == 1),
+                    )
+            st[("kp", i)] = kp
+            st[("kf", i)] = outp.tile([P, H, 4, NOPE + ROPE], F32, name="kf")
+            st[("vv", i)] = outp.tile([P, H, 4, VDIM], F32, name="vv")
+
+        def rope_mul(i):
+            pt = work.tile([P, 4, 2, 2, 64], F32, name="pt")
+            t0 = 4 * (i % 2)
+            nc.vector.tensor_tensor(
+                out=pt[:].rearrange("p t h r c -> p (t h) r c"),
+                in0=st[("kp", i)][:].rearrange("p t (h c) -> p (t h) c", h=2).unsqueeze(2).to_broadcast([P, 8, 2, 64]),
+                in1=cs[:, t0 : t0 + 4, :, :].rearrange("p t (h r) c -> p (t h) r c", h=2),
+                op=ALU.mult,
+            )
+            st[("pt", i)] = pt
+
+        def rope_add(i):
+            pt = st[("pt", i)]
+            nc.vector.tensor_tensor(
+                out=st[("kf", i)][:, 0, :, NOPE:].rearrange("p t (c r) -> p t c r", r=2),
+                in0=pt[:, :, 0, :, :].rearrange("p t r c -> p t c r"),
+                in1=pt[:, :, 1, :, :].rearrange("p t r c -> p t c r"),
+                op=ALU.add,
+            )
+
+        def rope_rep(i):
+            kf = st[("kf", i)]
+            nc.vector.tensor_copy(
+                out=kf[:, 1:H, :, NOPE:],
+                in_=kf[:, 0:1, :, NOPE:].to_broadcast([P, H - 1, 4, ROPE]),
+            )
+
+        def latent_mm(i, j):
+            ct = ps_ct.tile([P, 4, 128], F32, name="ct")
+            for m in range(4):
+                for g in range(2):
+                    nc.tensor.matmul_mx(
+                        out=ct[:, m, :],
+                        lhsT=wa_c[:, g, 128 * m : 128 * (m + 1)].bitcast(FP8X4),
+                        lhsT_scale=wa_s[:, g, 128 * m : 128 * (m + 1)],
+                        rhs=st[("xc", i)][:, x_cols(j, g)].bitcast(FP8X4),
+                        rhs_scale=st[("xs", i)][:, x_cols(j, g)],
+                        start=(g == 0),
+                        stop=(g == 1),
+                    )
+            st[("ct", i, j)] = ct
+            if j == 0:
+                st[("cg", i)] = work.tile([P, 512, 4], BF16, name="cg", align_bytes=64)
+
+        def c_out(i, j, eng):
+            dst = st[("cg", i)][:, 128 * j : 128 * (j + 1), :]
+            src = st[("ct", i, j)][:].rearrange("p m r -> p r m")
+            if eng == "s":
+                nc.scalar.copy(out=dst, in_=src)
+            else:
+                nc.vector.tensor_copy(out=dst, in_=src)
+
+        def quant_c(i):
+            st[("cc", i)] = work.tile([P, 512], U32, name="cc", align_bytes=64)
+            st[("cs", i)] = work.tile([P, 512], U8, name="cs_", align_bytes=64)
+            nc.vector.quantize_mx(
+                out=st[("cc", i)][:].bitcast(FP8X4),
+                scales=st[("cs", i)][:],
+                in_=st[("cg", i)][:].rearrange("p w t -> p (w t)"),
+            )
+
+        def kv_mm(i, j):
+            kv = ps_kv.tile([P, H, 2, 64], F32, name="kv")
+            nc.tensor.matmul_mx(
+                out=kv[:].rearrange("p h s c -> p (h s c)"),
+                lhsT=st[("cc", i)][:, 128 * j : 128 * (j + 1)].bitcast(FP8X4),
+                lhsT_scale=st[("cs", i)][:, 128 * j : 128 * (j + 1)],
+                rhs=wb_c[:].bitcast(FP8X4),
+                rhs_scale=wb_s[:],
+                start=True,
+                stop=True,
+            )
+            st[("kv", i, j)] = kv
+
+        def kv_out(i, j, eng):
+            kv = st[("kv", i, j)]
+            for dst, s in ((st[("kf", i)][:, :, j, 0:NOPE], 0), (st[("vv", i)][:, :, j, :], 1)):
+                if eng == "s":
+                    nc.scalar.copy(out=dst, in_=kv[:, :, s, :])
+                else:
+                    nc.vector.tensor_copy(out=dst, in_=kv[:, :, s, :])
+
+        def store(i, j_lo, j_n):
+            b = i // 2
+            t0 = 4 * (i % 2) + j_lo
+            nc.sync.dma_start(
+                out=out_0[b].rearrange("h (p t) f -> p h t f", t=8)[:, :, t0 : t0 + j_n, :],
+                in_=st[("kf", i)][:, :, j_lo : j_lo + j_n, :],
+            )
+            nc.sync.dma_start(
+                out=out_1[b].rearrange("h (p t) f -> p h t f", t=8)[:, :, t0 : t0 + j_n, :],
+                in_=st[("vv", i)][:, :, j_lo : j_lo + j_n, :],
+            )
+
+        transposes(0, 0)
+        transposes(0, 1)
+        transposes(0, 2)
+        x_out(0, 0, "s")
+        transposes(0, 3)
+        x_out(0, 1, "s")
+        quant_x(0, 0)
+        x_out(0, 2, "s")
+        x_out(0, 3, "s")
+        quant_rope_w()
+        quant_x(0, 1)
+        prep_wb()
+
+        for i in range(UNITS + 1):
+            nxt = i + 1 < UNITS
+            cur = i < UNITS
+            prv = i >= 1
+            last = i == UNITS
+            if nxt:
+                transposes(i + 1, 0)
+                transposes(i + 1, 1)
+                transposes(i + 1, 2)
+            if prv:
+                quant_c(i - 1)
+            if nxt:
+                x_out(i + 1, 0, "s")
+                transposes(i + 1, 3)
+                x_out(i + 1, 1, "s")
+                quant_x(i + 1, 0)
+                x_out(i + 1, 2, "s")
+                x_out(i + 1, 3, "s")
+            if cur:
+                rope_mm(i)
+                rope_mul(i)
+            for j in range(4):
+                if cur:
+                    latent_mm(i, j)
+                    c_out(i, j, "v" if j % 2 == 0 else "s")
+                if prv:
+                    kv_mm(i - 1, j)
+                    kv_out(i - 1, j, "v" if (last and j % 2 == 1) else "s")
+                if j == 0 and nxt:
+                    quant_x(i + 1, 1)
+                if j == 1 and cur:
+                    rope_add(i)
+                if last and j % 2 == 1:
+                    store(i - 1, j - 1, 2)
+            if cur:
+                rope_rep(i)
+            if prv and not last:
+                store(i - 1, 0, 4)

@@ -1,9 +1,7 @@
 import math
 from contextlib import ExitStack
 
-import concourse.bass as bass
 import concourse.mybir as mybir
-import concourse.tile as tile
 from concourse.masks import make_identity
 
 F32 = mybir.dt.float32
@@ -23,6 +21,58 @@ UNITS = 8
 FLOPS = 2 * B * N * E * WA + 2 * B * N * KVR * H * (NOPE + VDIM)
 MANUAL = True
 
+PROGRAM = (
+    ("LD", "wa0"), ("LD", "x0a"), ("LD", "wa1"), ("LD", "x0b"), ("LD", "wb"), ("LD", "x1"),
+    ("LD", "x2"), ("LD", "x3"), ("LD", "x4"), ("LD", "x5"), ("LD", "x6"), ("LD", "x7"),
+    ("IOTA",), ("IDENT",), ("SIN0",), ("TABV",), ("SIN2",), ("CSG",),
+    ("RGA", 0, "V", 0, 512), ("T", 0, 0), ("T", 0, 1), ("XO", 0, 0, "S"), ("XO", 0, 1, "S"), ("QWA", 0),
+    ("RGA", 1, "V", 0, 352), ("RGA", 1, "S", 352, 512), ("QX", 0, 0), ("QWA", 1), ("T", 0, 2), ("T", 0, 3),
+    ("RGR", 0, "S"), ("XO", 0, 2, "S"), ("XO", 0, 3, "S"), ("RGR", 1, "S"), ("QX", 0, 1), ("S1", 0, 0),
+    ("CO", 0, 0, "V"), ("S1", 0, 1), ("CO", 0, 1, "S"), ("QCP", 0, 0), ("S1", 0, 2), ("CO", 0, 2, "V"),
+    ("S1", 0, 3), ("CO", 0, 3, "S"), ("QWR",), ("RGB", "V", 0, 256), ("RGB", "S", 256, 512), ("QWB",),
+    ("QCP", 0, 1), ("R", 0), ("RM", 0), ("RA", 0, "G"), ("RR", 0, "G"), ("T", 1, 0),
+    ("T", 1, 1), ("T", 1, 2), ("XO", 1, 0, "S"), ("T", 1, 3), ("XO", 1, 1, "S"), ("QX", 1, 0),
+    ("XO", 1, 2, "S"), ("XO", 1, 3, "S"), ("S2", 0, 0), ("KO", 0, 0, "V"), ("QX", 1, 1), ("S2", 0, 1),
+    ("KO", 0, 1, "S"), ("T", 2, 0), ("T", 2, 1), ("T", 2, 2), ("XO", 2, 0, "S"), ("T", 2, 3),
+    ("XO", 2, 1, "S"), ("QX", 2, 0), ("XO", 2, 2, "S"), ("XO", 2, 3, "S"), ("S2", 0, 2), ("KO", 0, 2, "S"),
+    ("S2", 0, 3), ("KO", 0, 3, "S"), ("ST", 0, 0, 4), ("R", 1), ("RM", 1), ("S1", 1, 0),
+    ("CO", 1, 0, "V"), ("S1", 1, 1), ("CO", 1, 1, "S"), ("QCP", 1, 0), ("S1", 1, 2), ("CO", 1, 2, "V"),
+    ("QX", 2, 1), ("S1", 1, 3), ("CO", 1, 3, "S"), ("RA", 1, "G"), ("RR", 1, "G"), ("S2", 1, 0),
+    ("KO", 1, 0, "S"), ("S2", 1, 1), ("KO", 1, 1, "V"), ("T", 3, 0), ("T", 3, 1), ("T", 3, 2),
+    ("XO", 3, 0, "S"), ("T", 3, 3), ("XO", 3, 1, "S"), ("QCP", 1, 1), ("QX", 3, 0), ("XO", 3, 2, "S"),
+    ("XO", 3, 3, "S"), ("S2", 1, 2), ("KO", 1, 2, "S"), ("S2", 1, 3), ("KO", 1, 3, "S"), ("ST", 1, 0, 4),
+    ("R", 2), ("RM", 2), ("S1", 2, 0), ("CO", 2, 0, "V"), ("S1", 2, 1), ("CO", 2, 1, "S"),
+    ("QCP", 2, 0), ("S1", 2, 2), ("CO", 2, 2, "V"), ("QX", 3, 1), ("S1", 2, 3), ("CO", 2, 3, "S"),
+    ("RA", 2, "G"), ("RR", 2, "G"), ("S2", 2, 0), ("KO", 2, 0, "S"), ("S2", 2, 1), ("KO", 2, 1, "V"),
+    ("T", 4, 0), ("T", 4, 1), ("T", 4, 2), ("XO", 4, 0, "S"), ("T", 4, 3), ("XO", 4, 1, "S"),
+    ("QCP", 2, 1), ("QX", 4, 0), ("XO", 4, 2, "S"), ("XO", 4, 3, "S"), ("S2", 2, 2), ("KO", 2, 2, "S"),
+    ("S2", 2, 3), ("KO", 2, 3, "S"), ("ST", 2, 0, 4), ("R", 3), ("RM", 3), ("S1", 3, 0),
+    ("CO", 3, 0, "V"), ("S1", 3, 1), ("CO", 3, 1, "S"), ("QCP", 3, 0), ("S1", 3, 2), ("CO", 3, 2, "V"),
+    ("QX", 4, 1), ("S1", 3, 3), ("CO", 3, 3, "S"), ("RA", 3, "G"), ("RR", 3, "G"), ("S2", 3, 0),
+    ("KO", 3, 0, "S"), ("S2", 3, 1), ("KO", 3, 1, "V"), ("T", 5, 0), ("T", 5, 1), ("T", 5, 2),
+    ("XO", 5, 0, "S"), ("T", 5, 3), ("XO", 5, 1, "S"), ("QCP", 3, 1), ("QX", 5, 0), ("XO", 5, 2, "S"),
+    ("XO", 5, 3, "S"), ("S2", 3, 2), ("KO", 3, 2, "S"), ("S2", 3, 3), ("KO", 3, 3, "S"), ("ST", 3, 0, 4),
+    ("R", 4), ("RM", 4), ("S1", 4, 0), ("CO", 4, 0, "V"), ("S1", 4, 1), ("CO", 4, 1, "S"),
+    ("QCP", 4, 0), ("S1", 4, 2), ("CO", 4, 2, "V"), ("QX", 5, 1), ("S1", 4, 3), ("CO", 4, 3, "S"),
+    ("RA", 4, "G"), ("RR", 4, "G"), ("S2", 4, 0), ("KO", 4, 0, "S"), ("S2", 4, 1), ("KO", 4, 1, "V"),
+    ("T", 6, 0), ("T", 6, 1), ("T", 6, 2), ("XO", 6, 0, "S"), ("T", 6, 3), ("XO", 6, 1, "S"),
+    ("QCP", 4, 1), ("QX", 6, 0), ("XO", 6, 2, "S"), ("XO", 6, 3, "S"), ("S2", 4, 2), ("KO", 4, 2, "S"),
+    ("S2", 4, 3), ("KO", 4, 3, "S"), ("ST", 4, 0, 4), ("R", 5), ("RM", 5), ("S1", 5, 0),
+    ("CO", 5, 0, "V"), ("S1", 5, 1), ("CO", 5, 1, "S"), ("QCP", 5, 0), ("S1", 5, 2), ("CO", 5, 2, "V"),
+    ("QX", 6, 1), ("S1", 5, 3), ("CO", 5, 3, "S"), ("RA", 5, "G"), ("RR", 5, "G"), ("S2", 5, 0),
+    ("KO", 5, 0, "S"), ("S2", 5, 1), ("KO", 5, 1, "V"), ("T", 7, 0), ("T", 7, 1), ("T", 7, 2),
+    ("XO", 7, 0, "S"), ("T", 7, 3), ("XO", 7, 1, "S"), ("QCP", 5, 1), ("QX", 7, 0), ("XO", 7, 2, "S"),
+    ("XO", 7, 3, "S"), ("S2", 5, 2), ("KO", 5, 2, "S"), ("S2", 5, 3), ("KO", 5, 3, "S"), ("ST", 5, 0, 4),
+    ("R", 6), ("RM", 6), ("S1", 6, 0), ("CO", 6, 0, "V"), ("S1", 6, 1), ("CO", 6, 1, "S"),
+    ("QCP", 6, 0), ("S1", 6, 2), ("CO", 6, 2, "V"), ("QX", 7, 1), ("S1", 6, 3), ("CO", 6, 3, "S"),
+    ("RA", 6, "G"), ("RR", 6, "G"), ("S2", 6, 0), ("KO", 6, 0, "S"), ("S2", 6, 1), ("KO", 6, 1, "V"),
+    ("QCP", 6, 1), ("S2", 6, 2), ("KO", 6, 2, "S"), ("S2", 6, 3), ("KO", 6, 3, "S"), ("ST", 6, 0, 4),
+    ("R", 7), ("RM", 7), ("S1", 7, 0), ("CO", 7, 0, "V"), ("S1", 7, 1), ("CO", 7, 1, "S"),
+    ("QCP", 7, 0), ("S1", 7, 2), ("CO", 7, 2, "V"), ("S1", 7, 3), ("CO", 7, 3, "S"), ("RA", 7, "G"),
+    ("RR", 7, "G"), ("S2", 7, 0), ("KO", 7, 0, "S"), ("S2", 7, 1), ("KO", 7, 1, "V"), ("QCP", 7, 1),
+    ("S2", 7, 2), ("KO", 7, 2, "S"), ("ST", 7, 0, 3), ("S2", 7, 3), ("KO", 7, 3, "V"), ("ST", 7, 3, 1),
+)
+
 
 def tile_multilatentattention_pb_t_kernel(tc, x, Wkva, Wkvb, out_0, out_1):
     nc = tc.nc
@@ -33,114 +83,104 @@ def tile_multilatentattention_pb_t_kernel(tc, x, Wkva, Wkvb, out_0, out_1):
         work = ctx.enter_context(tc.tile_pool(name="work", bufs=2))
         outp = ctx.enter_context(tc.tile_pool(name="outp", bufs=3))
         ps_xt = ctx.enter_context(tc.psum_pool(name="ps_xt", bufs=3))
-        ps_ct = ctx.enter_context(tc.psum_pool(name="ps_ct", bufs=2))
+        ps_mx = ctx.enter_context(tc.psum_pool(name="ps_mx", bufs=3))
         ps_kv = ctx.enter_context(tc.psum_pool(name="ps_kv", bufs=2))
-        ps_kp = ctx.enter_context(tc.psum_pool(name="ps_kp", bufs=1))
 
         wa_raw = const.tile([P, 2, 4, WA], BF16)
-        for g in range(2):
-            nc.sync.dma_start(
-                out=wa_raw[:, g, :, :].rearrange("p (u e) c -> p u (e c)", e=2),
-                in_=Wkva[512 * g : 512 * (g + 1), :].rearrange("(u q e) c -> q u (e c)", u=2, e=2),
-            )
+        wb_raw = const.tile([P, 4, 512], BF16)
         x_sb = []
         for i in range(UNITS):
             x_sb.append(const.tile([P, 4, E], BF16, name="x_sb%d" % i))
-        wb_raw = const.tile([P, 4, 512], BF16)
-
-        def load_x(i, t_lo, t_n):
-            src = x[i // 2].rearrange("(p t) k -> p t k", t=8)
-            t0 = 4 * (i % 2)
-            nc.sync.dma_start(out=x_sb[i][:, t_lo : t_lo + t_n, :], in_=src[:, t0 + t_lo : t0 + t_lo + t_n, :])
-
-        load_x(0, 0, 2)
-        load_x(0, 2, 2)
-        load_x(1, 0, 4)
-        nc.sync.dma_start(out=wb_raw[:], in_=Wkvb.rearrange("(t p) n -> p t n", p=P))
-        for i in range(2, UNITS):
-            load_x(i, 0, 4)
-
         ident = const.tile([P, P], F32)
-        make_identity(nc, ident[:])
         n_i = const.tile([P, 8], I32)
-        nc.gpsimd.iota(out=n_i[:], pattern=[[1, 8]], base=0, channel_multiplier=8)
-
-        ab = const.tile([P, 16], F32)
-        one = const.tile([P, 1], F32)
-        nc.vector.memset(one[:], 1.0)
-        for a in range(8):
-            nc.vector.tensor_scalar_mul(out=ab[:, a : a + 1], in0=one[:], scalar1=BASE ** (-2.0 * 8 * a / ROPE) / (2.0 * math.pi))
-        for b in range(8):
-            nc.vector.tensor_scalar_mul(out=ab[:, 8 + b : 9 + b], in0=one[:], scalar1=BASE ** (-2.0 * b / ROPE))
-        u_t = const.tile([P, 8, 8], F32)
-        nc.vector.tensor_tensor(
-            out=u_t[:],
-            in0=ab[:, 0:8].unsqueeze(2).to_broadcast([P, 8, 8]),
-            in1=ab[:, 8:16].unsqueeze(1).to_broadcast([P, 8, 8]),
-            op=ALU.mult,
-        )
         n_f = const.tile([P, 8], F32)
-        nc.vector.tensor_copy(out=n_f[:], in_=n_i[:])
+        one = const.tile([P, 1], F32)
+        junk = const.tile([P, 1], F32)
+        u_t = const.tile([P, 64], F32)
         t_a = const.tile([P, 8, 64], F32)
         t_b = const.tile([P, 8, 64], F32)
         t_k = const.tile([P, 8, 64], I32)
-        nc.vector.tensor_tensor(
-            out=t_a[:],
-            in0=n_f[:].unsqueeze(2).to_broadcast([P, 8, 64]),
-            in1=u_t[:].rearrange("p a b -> p (a b)").unsqueeze(1).to_broadcast([P, 8, 64]),
-            op=ALU.mult,
-        )
-        nc.vector.tensor_copy(out=t_k[:], in_=t_a[:])
-        nc.vector.tensor_copy(out=t_b[:], in_=t_k[:])
-        nc.vector.tensor_tensor(out=t_a[:], in0=t_a[:], in1=t_b[:], op=ALU.subtract)
-        nc.vector.scalar_tensor_tensor(out=t_b[:], in0=t_a[:], scalar=0.5, in1=t_a[:], op0=ALU.is_gt, op1=ALU.subtract)
-        nc.vector.scalar_tensor_tensor(out=t_a[:], in0=t_b[:], scalar=-1.0, in1=t_b[:], op0=ALU.mult, op1=ALU.min)
-        nc.vector.tensor_scalar_add(out=t_a[:], in0=t_a[:], scalar1=0.25)
         cs = const.tile([P, 8, 4, 64], F32)
-        nc.scalar.activation(out=cs[:, :, 0, :], in_=t_a[:], func=ACT.Sin, scale=2.0 * math.pi)
-        nc.scalar.activation(out=cs[:, :, 1, :], in_=t_b[:], func=ACT.Sin, scale=-2.0 * math.pi)
-        nc.scalar.activation(out=cs[:, :, 2, :], in_=t_b[:], func=ACT.Sin, scale=2.0 * math.pi)
-        nc.scalar.activation(out=cs[:, :, 3, :], in_=t_a[:], func=ACT.Sin, scale=2.0 * math.pi)
-
         wa_g = const.tile([P, 2, WA, 4], BF16, align_bytes=64)
         wa_c = const.tile([P, 2, WA], U32, align_bytes=64)
         wa_s = const.tile([P, 2, WA], U8, align_bytes=64)
-        for g in range(2):
-            nc.vector.tensor_copy(
-                out=wa_g[:, g, 0:KVR, :].rearrange("p (c i) t -> p c t i", i=4),
-                in_=wa_raw[:, g, :, 0:KVR].rearrange("p t (c i) -> p c t i", i=4),
-            )
-            nc.scalar.copy(
-                out=wa_g[:, g, KVR:WA, :].rearrange("p (h i) t -> p h i t", h=2),
-                in_=wa_raw[:, g, :, KVR:WA].rearrange("p t (i h) -> p h i t", h=2),
-            )
-        for g in range(2):
-            nc.vector.quantize_mx(
-                out=wa_c[:, g, 0:KVR].bitcast(FP8X4),
-                scales=wa_s[:, g, 0:KVR],
-                in_=wa_g[:, g, 0:KVR, :].rearrange("p w t -> p (w t)"),
-            )
-
-        def quant_rope_w():
-            for g in range(2):
-                nc.vector.quantize_mx(
-                    out=wa_c[:, g, KVR:WA].bitcast(FP8X4),
-                    scales=wa_s[:, g, KVR:WA],
-                    in_=wa_g[:, g, KVR:WA, :].rearrange("p w t -> p (w t)"),
-                )
-
         wb_g = const.tile([P, 512, 4], BF16, align_bytes=64)
         wb_c = const.tile([P, 512], U32, align_bytes=64)
         wb_s = const.tile([P, 512], U8, align_bytes=64)
-
-        def prep_wb():
-            nc.vector.tensor_copy(
-                out=wb_g[:].rearrange("p (c i) t -> p c t i", i=4),
-                in_=wb_raw[:].rearrange("p t (c i) -> p c t i", i=4),
-            )
-            nc.vector.quantize_mx(out=wb_c[:].bitcast(FP8X4), scales=wb_s[:], in_=wb_g[:].rearrange("p w t -> p (w t)"))
-
         st = {}
+
+        def copy(eng, out, in_):
+            if eng == "S":
+                nc.scalar.copy(out=out, in_=in_)
+            elif eng == "V":
+                nc.vector.tensor_copy(out=out, in_=in_)
+            else:
+                nc.gpsimd.tensor_scalar(out=out, in0=in_, scalar1=1.0, scalar2=0.0, op0=ALU.mult, op1=ALU.add)
+
+        def load(what):
+            if what == "wa0" or what == "wa1":
+                g = 0 if what == "wa0" else 1
+                nc.sync.dma_start(
+                    out=wa_raw[:, g, :, :].rearrange("p (u e) c -> p u (e c)", e=2),
+                    in_=Wkva[512 * g : 512 * (g + 1), :].rearrange("(u q e) c -> q u (e c)", u=2, e=2),
+                )
+            elif what == "wb":
+                nc.sync.dma_start(out=wb_raw[:], in_=Wkvb.rearrange("(t p) n -> p t n", p=P))
+            else:
+                i = int(what[1])
+                lo, n = 0, 4
+                if len(what) == 3:
+                    lo, n = (0, 2) if what[2] == "a" else (2, 2)
+                src = x[i // 2].rearrange("(p t) k -> p t k", t=8)
+                t0 = 4 * (i % 2) + lo
+                nc.sync.dma_start(out=x_sb[i][:, lo : lo + n, :], in_=src[:, t0 : t0 + n, :])
+
+        def tables():
+            nc.vector.tensor_scalar_mul(out=u_t[:, 0:1], in0=one[:], scalar1=1.0 / (2.0 * math.pi))
+            s = 1
+            while s < 64:
+                nc.vector.tensor_scalar_mul(out=u_t[:, s : 2 * s], in0=u_t[:, 0:s], scalar1=BASE ** (-2.0 * s / ROPE))
+                s *= 2
+            nc.vector.tensor_copy(out=n_f[:], in_=n_i[:])
+            nc.vector.tensor_tensor(
+                out=t_a[:],
+                in0=n_f[:].unsqueeze(2).to_broadcast([P, 8, 64]),
+                in1=u_t[:].unsqueeze(1).to_broadcast([P, 8, 64]),
+                op=ALU.mult,
+            )
+            nc.vector.tensor_copy(out=t_k[:], in_=t_a[:])
+            nc.vector.tensor_tensor(out=t_a[:], in0=t_a[:], in1=t_k[:], op=ALU.subtract)
+            nc.vector.scalar_tensor_tensor(out=t_b[:], in0=t_a[:], scalar=0.5, in1=t_a[:], op0=ALU.is_gt, op1=ALU.subtract)
+            nc.vector.scalar_tensor_tensor(out=t_a[:], in0=t_b[:], scalar=-1.0, in1=t_b[:], op0=ALU.mult, op1=ALU.min)
+            nc.vector.tensor_scalar_add(out=t_a[:], in0=t_a[:], scalar1=0.25)
+
+        def regroup_a(g, eng, lo, hi):
+            copy(
+                eng,
+                wa_g[:, g, lo:hi, :].rearrange("p (c i) t -> p c t i", i=4),
+                wa_raw[:, g, :, lo:hi].rearrange("p t (c i) -> p c t i", i=4),
+            )
+
+        def regroup_r(g, eng):
+            copy(
+                eng,
+                wa_g[:, g, KVR:WA, :].rearrange("p (h i) t -> p h i t", h=2),
+                wa_raw[:, g, :, KVR:WA].rearrange("p t (i h) -> p h i t", h=2),
+            )
+
+        def quant_w(g, lo, hi):
+            nc.vector.quantize_mx(
+                out=wa_c[:, g, lo:hi].bitcast(FP8X4),
+                scales=wa_s[:, g, lo:hi],
+                in_=wa_g[:, g, lo:hi, :].rearrange("p w t -> p (w t)"),
+            )
+
+        def regroup_b(eng, lo, hi):
+            copy(
+                eng,
+                wb_g[:, lo:hi, :].rearrange("p (c i) t -> p c t i", i=4),
+                wb_raw[:, :, lo:hi].rearrange("p t (c i) -> p c t i", i=4),
+            )
 
         def transposes(i, q):
             pr, g = q // 2, q % 2
@@ -160,13 +200,11 @@ def tile_multilatentattention_pb_t_kernel(tc, x, Wkva, Wkvb, out_0, out_1):
                 st[("xs", i)] = work.tile([P, 1024], U8, name="xs", align_bytes=64)
 
         def x_out(i, q, eng):
-            xg = st[("xg", i)]
-            dst = xg[:, 512 * q : 512 * (q + 1)].rearrange("p (r u) -> p r u", u=2)
-            src = st[("xt", i, q)][:].rearrange("p u r -> p r u")
-            if eng == "s":
-                nc.scalar.copy(out=dst, in_=src)
-            else:
-                nc.vector.tensor_copy(out=dst, in_=src)
+            copy(
+                eng,
+                st[("xg", i)][:, 512 * q : 512 * (q + 1)].rearrange("p (r u) -> p r u", u=2),
+                st[("xt", i, q)][:].rearrange("p u r -> p r u"),
+            )
 
         def quant_x(i, pr):
             nc.vector.quantize_mx(
@@ -180,7 +218,7 @@ def tile_multilatentattention_pb_t_kernel(tc, x, Wkva, Wkvb, out_0, out_1):
             return slice(c0, c0 + 128)
 
         def rope_mm(i):
-            kp = ps_kp.tile([P, 4, ROPE], F32, name="kp")
+            kp = ps_mx.tile([P, 4, 128], F32, name="mx")
             for j in range(4):
                 for g in range(2):
                     nc.tensor.matmul_mx(
@@ -207,24 +245,26 @@ def tile_multilatentattention_pb_t_kernel(tc, x, Wkva, Wkvb, out_0, out_1):
             )
             st[("pt", i)] = pt
 
-        def rope_add(i):
+        def rope_add(i, eng):
             pt = st[("pt", i)]
-            nc.vector.tensor_tensor(
+            e = nc.gpsimd if eng == "G" else nc.vector
+            e.tensor_tensor(
                 out=st[("kf", i)][:, 0, :, NOPE:].rearrange("p t (c r) -> p t c r", r=2),
                 in0=pt[:, :, 0, :, :].rearrange("p t r c -> p t c r"),
                 in1=pt[:, :, 1, :, :].rearrange("p t r c -> p t c r"),
                 op=ALU.add,
             )
 
-        def rope_rep(i):
+        def rope_rep(i, eng):
             kf = st[("kf", i)]
-            nc.vector.tensor_copy(
-                out=kf[:, 1:H, :, NOPE:],
-                in_=kf[:, 0:1, :, NOPE:].to_broadcast([P, H - 1, 4, ROPE]),
-            )
+            if eng == "G":
+                for h in range(1, H):
+                    copy("G", kf[:, h, :, NOPE:], kf[:, 0, :, NOPE:])
+            else:
+                copy(eng, kf[:, 1:H, :, NOPE:], kf[:, 0:1, :, NOPE:].to_broadcast([P, H - 1, 4, ROPE]))
 
         def latent_mm(i, j):
-            ct = ps_ct.tile([P, 4, 128], F32, name="ct")
+            ct = ps_mx.tile([P, 4, 128], F32, name="mx")
             for m in range(4):
                 for g in range(2):
                     nc.tensor.matmul_mx(
@@ -241,20 +281,16 @@ def tile_multilatentattention_pb_t_kernel(tc, x, Wkva, Wkvb, out_0, out_1):
                 st[("cg", i)] = work.tile([P, 512, 4], BF16, name="cg", align_bytes=64)
 
         def c_out(i, j, eng):
-            dst = st[("cg", i)][:, 128 * j : 128 * (j + 1), :]
-            src = st[("ct", i, j)][:].rearrange("p m r -> p r m")
-            if eng == "s":
-                nc.scalar.copy(out=dst, in_=src)
-            else:
-                nc.vector.tensor_copy(out=dst, in_=src)
+            copy(eng, st[("cg", i)][:, 128 * j : 128 * (j + 1), :], st[("ct", i, j)][:].rearrange("p m r -> p r m"))
 
-        def quant_c(i):
-            st[("cc", i)] = work.tile([P, 512], U32, name="cc", align_bytes=64)
-            st[("cs", i)] = work.tile([P, 512], U8, name="cs_", align_bytes=64)
+        def quant_c(i, pr):
+            if pr == 0:
+                st[("cc", i)] = work.tile([P, 512], U32, name="cc", align_bytes=64)
+                st[("cs", i)] = work.tile([P, 512], U8, name="csc", align_bytes=64)
             nc.vector.quantize_mx(
-                out=st[("cc", i)][:].bitcast(FP8X4),
-                scales=st[("cs", i)][:],
-                in_=st[("cg", i)][:].rearrange("p w t -> p (w t)"),
+                out=st[("cc", i)][:, 256 * pr : 256 * (pr + 1)].bitcast(FP8X4),
+                scales=st[("cs", i)][:, 256 * pr : 256 * (pr + 1)],
+                in_=st[("cg", i)][:, 256 * pr : 256 * (pr + 1), :].rearrange("p w t -> p (w t)"),
             )
 
         def kv_mm(i, j):
@@ -272,11 +308,8 @@ def tile_multilatentattention_pb_t_kernel(tc, x, Wkva, Wkvb, out_0, out_1):
 
         def kv_out(i, j, eng):
             kv = st[("kv", i, j)]
-            for dst, s in ((st[("kf", i)][:, :, j, 0:NOPE], 0), (st[("vv", i)][:, :, j, :], 1)):
-                if eng == "s":
-                    nc.scalar.copy(out=dst, in_=kv[:, :, s, :])
-                else:
-                    nc.vector.tensor_copy(out=dst, in_=kv[:, :, s, :])
+            copy(eng, st[("kf", i)][:, :, j, 0:NOPE], kv[:, :, 0, :])
+            copy(eng, st[("vv", i)][:, :, j, :], kv[:, :, 1, :])
 
         def store(i, j_lo, j_n):
             b = i // 2
@@ -290,54 +323,63 @@ def tile_multilatentattention_pb_t_kernel(tc, x, Wkva, Wkvb, out_0, out_1):
                 in_=st[("vv", i)][:, :, j_lo : j_lo + j_n, :],
             )
 
-        transposes(0, 0)
-        transposes(0, 1)
-        transposes(0, 2)
-        x_out(0, 0, "s")
-        transposes(0, 3)
-        x_out(0, 1, "s")
-        quant_x(0, 0)
-        x_out(0, 2, "s")
-        x_out(0, 3, "s")
-        quant_rope_w()
-        quant_x(0, 1)
-        prep_wb()
-
-        for i in range(UNITS + 1):
-            nxt = i + 1 < UNITS
-            cur = i < UNITS
-            prv = i >= 1
-            last = i == UNITS
-            if nxt:
-                transposes(i + 1, 0)
-                transposes(i + 1, 1)
-                transposes(i + 1, 2)
-            if prv:
-                quant_c(i - 1)
-            if nxt:
-                x_out(i + 1, 0, "s")
-                transposes(i + 1, 3)
-                x_out(i + 1, 1, "s")
-                quant_x(i + 1, 0)
-                x_out(i + 1, 2, "s")
-                x_out(i + 1, 3, "s")
-            if cur:
-                rope_mm(i)
-                rope_mul(i)
-            for j in range(4):
-                if cur:
-                    latent_mm(i, j)
-                    c_out(i, j, "v" if j % 2 == 0 else "s")
-                if prv:
-                    kv_mm(i - 1, j)
-                    kv_out(i - 1, j, "v" if (last and j % 2 == 1) else "s")
-                if j == 0 and nxt:
-                    quant_x(i + 1, 1)
-                if j == 1 and cur:
-                    rope_add(i)
-                if last and j % 2 == 1:
-                    store(i - 1, j - 1, 2)
-            if cur:
-                rope_rep(i)
-            if prv and not last:
-                store(i - 1, 0, 4)
+        for t in PROGRAM:
+            k = t[0]
+            if k == "LD":
+                load(t[1])
+            elif k == "IOTA":
+                nc.gpsimd.iota(out=n_i[:], pattern=[[1, 8]], base=0, channel_multiplier=8)
+            elif k == "IDENT":
+                make_identity(nc, ident[:])
+            elif k == "SIN0":
+                nc.vector.memset(one[:], 1.0)
+                nc.scalar.activation(out=junk[:], in_=one[:], func=ACT.Sin)
+            elif k == "TABV":
+                tables()
+            elif k == "SIN2":
+                nc.scalar.activation(out=cs[:, :, 0, :], in_=t_a[:], func=ACT.Sin, scale=2.0 * math.pi)
+                nc.scalar.activation(out=cs[:, :, 1, :], in_=t_b[:], func=ACT.Sin, scale=-2.0 * math.pi)
+            elif k == "CSG":
+                nc.gpsimd.tensor_scalar(out=cs[:, :, 2, :], in0=cs[:, :, 1, :], scalar1=-1.0, scalar2=0.0, op0=ALU.mult, op1=ALU.add)
+                copy("G", cs[:, :, 3, :], cs[:, :, 0, :])
+            elif k == "RGA":
+                regroup_a(t[1], t[2], t[3], t[4])
+            elif k == "RGR":
+                regroup_r(t[1], t[2])
+            elif k == "QWA":
+                quant_w(t[1], 0, KVR)
+            elif k == "QWR":
+                quant_w(0, KVR, WA)
+                quant_w(1, KVR, WA)
+            elif k == "RGB":
+                regroup_b(t[1], t[2], t[3])
+            elif k == "QWB":
+                nc.vector.quantize_mx(out=wb_c[:].bitcast(FP8X4), scales=wb_s[:], in_=wb_g[:].rearrange("p w t -> p (w t)"))
+            elif k == "T":
+                transposes(t[1], t[2])
+            elif k == "XO":
+                x_out(t[1], t[2], t[3])
+            elif k == "QX":
+                quant_x(t[1], t[2])
+            elif k == "R":
+                rope_mm(t[1])
+            elif k == "RM":
+                rope_mul(t[1])
+            elif k == "RA":
+                rope_add(t[1], t[2])
+            elif k == "RR":
+                rope_rep(t[1], t[2])
+            elif k == "S1":
+                latent_mm(t[1], t[2])
+            elif k == "CO":
+                c_out(t[1], t[2], t[3])
+            elif k == "QCP":
+                quant_c(t[1], t[2])
+            elif k == "S2":
+                kv_mm(t[1], t[2])
+            elif k == "KO":
+                kv_out(t[1], t[2], t[3])
+            elif k == "ST":
+                store(t[1], t[2], t[3])
+            else:
+                raise ValueError(k)

@@ -19,66 +19,12 @@ BASE = 10000.0
 WA = KVR + ROPE
 UNITS = 8
 FLOPS = 2 * B * N * E * WA + 2 * B * N * KVR * H * (NOPE + VDIM)
-MANUAL = True
-
-PROGRAM = (
-    ("LD", "wa0"), ("LD", "x0a"), ("LD", "wa1"), ("LD", "x0b"), ("LD", "wb"), ("LD", "x1"),
-    ("LD", "x2"), ("LD", "x3"), ("LD", "x4"), ("LD", "x5"), ("LD", "x6"), ("LD", "x7"),
-    ("IOTA",), ("IDENT",), ("SIN0",), ("TABV",), ("SIN2",), ("CSG",),
-    ("RGA", 0, "V", 0, 512), ("T", 0, 0), ("T", 0, 1), ("XO", 0, 0, "S"), ("XO", 0, 1, "S"), ("QWA", 0),
-    ("RGA", 1, "V", 0, 352), ("RGA", 1, "S", 352, 512), ("QX", 0, 0), ("QWA", 1), ("T", 0, 2), ("T", 0, 3),
-    ("RGR", 0, "S"), ("XO", 0, 2, "S"), ("XO", 0, 3, "S"), ("RGR", 1, "S"), ("QX", 0, 1), ("S1", 0, 0),
-    ("CO", 0, 0, "V"), ("S1", 0, 1), ("CO", 0, 1, "S"), ("QCP", 0, 0), ("S1", 0, 2), ("CO", 0, 2, "V"),
-    ("S1", 0, 3), ("CO", 0, 3, "S"), ("QWR",), ("RGB", "V", 0, 256), ("RGB", "S", 256, 512), ("QWB",),
-    ("QCP", 0, 1), ("R", 0), ("RM", 0), ("RA", 0, "G"), ("RR", 0, "G"), ("T", 1, 0),
-    ("T", 1, 1), ("T", 1, 2), ("XO", 1, 0, "S"), ("T", 1, 3), ("XO", 1, 1, "S"), ("QX", 1, 0),
-    ("XO", 1, 2, "S"), ("XO", 1, 3, "S"), ("S2", 0, 0), ("KO", 0, 0, "V"), ("QX", 1, 1), ("S2", 0, 1),
-    ("KO", 0, 1, "S"), ("T", 2, 0), ("T", 2, 1), ("T", 2, 2), ("XO", 2, 0, "S"), ("T", 2, 3),
-    ("XO", 2, 1, "S"), ("QX", 2, 0), ("XO", 2, 2, "S"), ("XO", 2, 3, "S"), ("S2", 0, 2), ("KO", 0, 2, "S"),
-    ("S2", 0, 3), ("KO", 0, 3, "S"), ("ST", 0, 0, 4), ("R", 1), ("RM", 1), ("S1", 1, 0),
-    ("CO", 1, 0, "V"), ("S1", 1, 1), ("CO", 1, 1, "S"), ("QCP", 1, 0), ("S1", 1, 2), ("CO", 1, 2, "V"),
-    ("QX", 2, 1), ("S1", 1, 3), ("CO", 1, 3, "S"), ("RA", 1, "G"), ("RR", 1, "G"), ("S2", 1, 0),
-    ("KO", 1, 0, "S"), ("S2", 1, 1), ("KO", 1, 1, "V"), ("T", 3, 0), ("T", 3, 1), ("T", 3, 2),
-    ("XO", 3, 0, "S"), ("T", 3, 3), ("XO", 3, 1, "S"), ("QCP", 1, 1), ("QX", 3, 0), ("XO", 3, 2, "S"),
-    ("XO", 3, 3, "S"), ("S2", 1, 2), ("KO", 1, 2, "S"), ("S2", 1, 3), ("KO", 1, 3, "S"), ("ST", 1, 0, 4),
-    ("R", 2), ("RM", 2), ("S1", 2, 0), ("CO", 2, 0, "V"), ("S1", 2, 1), ("CO", 2, 1, "S"),
-    ("QCP", 2, 0), ("S1", 2, 2), ("CO", 2, 2, "V"), ("QX", 3, 1), ("S1", 2, 3), ("CO", 2, 3, "S"),
-    ("RA", 2, "G"), ("RR", 2, "G"), ("S2", 2, 0), ("KO", 2, 0, "S"), ("S2", 2, 1), ("KO", 2, 1, "V"),
-    ("T", 4, 0), ("T", 4, 1), ("T", 4, 2), ("XO", 4, 0, "S"), ("T", 4, 3), ("XO", 4, 1, "S"),
-    ("QCP", 2, 1), ("QX", 4, 0), ("XO", 4, 2, "S"), ("XO", 4, 3, "S"), ("S2", 2, 2), ("KO", 2, 2, "S"),
-    ("S2", 2, 3), ("KO", 2, 3, "S"), ("ST", 2, 0, 4), ("R", 3), ("RM", 3), ("S1", 3, 0),
-    ("CO", 3, 0, "V"), ("S1", 3, 1), ("CO", 3, 1, "S"), ("QCP", 3, 0), ("S1", 3, 2), ("CO", 3, 2, "V"),
-    ("QX", 4, 1), ("S1", 3, 3), ("CO", 3, 3, "S"), ("RA", 3, "G"), ("RR", 3, "G"), ("S2", 3, 0),
-    ("KO", 3, 0, "S"), ("S2", 3, 1), ("KO", 3, 1, "V"), ("T", 5, 0), ("T", 5, 1), ("T", 5, 2),
-    ("XO", 5, 0, "S"), ("T", 5, 3), ("XO", 5, 1, "S"), ("QCP", 3, 1), ("QX", 5, 0), ("XO", 5, 2, "S"),
-    ("XO", 5, 3, "S"), ("S2", 3, 2), ("KO", 3, 2, "S"), ("S2", 3, 3), ("KO", 3, 3, "S"), ("ST", 3, 0, 4),
-    ("R", 4), ("RM", 4), ("S1", 4, 0), ("CO", 4, 0, "V"), ("S1", 4, 1), ("CO", 4, 1, "S"),
-    ("QCP", 4, 0), ("S1", 4, 2), ("CO", 4, 2, "V"), ("QX", 5, 1), ("S1", 4, 3), ("CO", 4, 3, "S"),
-    ("RA", 4, "G"), ("RR", 4, "G"), ("S2", 4, 0), ("KO", 4, 0, "S"), ("S2", 4, 1), ("KO", 4, 1, "V"),
-    ("T", 6, 0), ("T", 6, 1), ("T", 6, 2), ("XO", 6, 0, "S"), ("T", 6, 3), ("XO", 6, 1, "S"),
-    ("QCP", 4, 1), ("QX", 6, 0), ("XO", 6, 2, "S"), ("XO", 6, 3, "S"), ("S2", 4, 2), ("KO", 4, 2, "S"),
-    ("S2", 4, 3), ("KO", 4, 3, "S"), ("ST", 4, 0, 4), ("R", 5), ("RM", 5), ("S1", 5, 0),
-    ("CO", 5, 0, "V"), ("S1", 5, 1), ("CO", 5, 1, "S"), ("QCP", 5, 0), ("S1", 5, 2), ("CO", 5, 2, "V"),
-    ("QX", 6, 1), ("S1", 5, 3), ("CO", 5, 3, "S"), ("RA", 5, "G"), ("RR", 5, "G"), ("S2", 5, 0),
-    ("KO", 5, 0, "S"), ("S2", 5, 1), ("KO", 5, 1, "V"), ("T", 7, 0), ("T", 7, 1), ("T", 7, 2),
-    ("XO", 7, 0, "S"), ("T", 7, 3), ("XO", 7, 1, "S"), ("QCP", 5, 1), ("QX", 7, 0), ("XO", 7, 2, "S"),
-    ("XO", 7, 3, "S"), ("S2", 5, 2), ("KO", 5, 2, "S"), ("S2", 5, 3), ("KO", 5, 3, "S"), ("ST", 5, 0, 4),
-    ("R", 6), ("RM", 6), ("S1", 6, 0), ("CO", 6, 0, "V"), ("S1", 6, 1), ("CO", 6, 1, "S"),
-    ("QCP", 6, 0), ("S1", 6, 2), ("CO", 6, 2, "V"), ("QX", 7, 1), ("S1", 6, 3), ("CO", 6, 3, "S"),
-    ("RA", 6, "G"), ("RR", 6, "G"), ("S2", 6, 0), ("KO", 6, 0, "S"), ("S2", 6, 1), ("KO", 6, 1, "V"),
-    ("QCP", 6, 1), ("S2", 6, 2), ("KO", 6, 2, "S"), ("S2", 6, 3), ("KO", 6, 3, "S"), ("ST", 6, 0, 4),
-    ("R", 7), ("RM", 7), ("S1", 7, 0), ("CO", 7, 0, "V"), ("S1", 7, 1), ("CO", 7, 1, "S"),
-    ("QCP", 7, 0), ("S1", 7, 2), ("CO", 7, 2, "V"), ("S1", 7, 3), ("CO", 7, 3, "S"), ("RA", 7, "G"),
-    ("RR", 7, "G"), ("S2", 7, 0), ("KO", 7, 0, "S"), ("S2", 7, 1), ("KO", 7, 1, "V"), ("QCP", 7, 1),
-    ("S2", 7, 2), ("KO", 7, 2, "S"), ("ST", 7, 0, 3), ("S2", 7, 3), ("KO", 7, 3, "V"), ("ST", 7, 3, 1),
-)
 
 
 def tile_multilatentattention_pb_t_kernel(tc, x, Wkva, Wkvb, out_0, out_1):
     nc = tc.nc
     with ExitStack() as ctx:
-        if MANUAL:
-            ctx.enter_context(tc.manual_schedule())
+        ctx.enter_context(tc.manual_schedule())
         const = ctx.enter_context(tc.tile_pool(name="const", bufs=1))
         work = ctx.enter_context(tc.tile_pool(name="work", bufs=2))
         outp = ctx.enter_context(tc.tile_pool(name="outp", bufs=3))
@@ -112,28 +58,19 @@ def tile_multilatentattention_pb_t_kernel(tc, x, Wkva, Wkvb, out_0, out_1):
         def copy(eng, out, in_):
             if eng == "S":
                 nc.scalar.copy(out=out, in_=in_)
-            elif eng == "V":
+            else:
                 nc.vector.tensor_copy(out=out, in_=in_)
-            else:
-                nc.gpsimd.tensor_scalar(out=out, in0=in_, scalar1=1.0, scalar2=0.0, op0=ALU.mult, op1=ALU.add)
 
-        def load(what):
-            if what == "wa0" or what == "wa1":
-                g = 0 if what == "wa0" else 1
-                nc.sync.dma_start(
-                    out=wa_raw[:, g, :, :].rearrange("p (u e) c -> p u (e c)", e=2),
-                    in_=Wkva[512 * g : 512 * (g + 1), :].rearrange("(u q e) c -> q u (e c)", u=2, e=2),
-                )
-            elif what == "wb":
-                nc.sync.dma_start(out=wb_raw[:], in_=Wkvb.rearrange("(t p) n -> p t n", p=P))
-            else:
-                i = int(what[1])
-                lo, n = 0, 4
-                if len(what) == 3:
-                    lo, n = (0, 2) if what[2] == "a" else (2, 2)
-                src = x[i // 2].rearrange("(p t) k -> p t k", t=8)
-                t0 = 4 * (i % 2) + lo
-                nc.sync.dma_start(out=x_sb[i][:, lo : lo + n, :], in_=src[:, t0 : t0 + n, :])
+        def load_wa(g):
+            nc.sync.dma_start(
+                out=wa_raw[:, g, :, :].rearrange("p (u e) c -> p u (e c)", e=2),
+                in_=Wkva[512 * g : 512 * (g + 1), :].rearrange("(u q e) c -> q u (e c)", u=2, e=2),
+            )
+
+        def load_x(i, lo, n):
+            src = x[i // 2].rearrange("(p t) k -> p t k", t=8)
+            t0 = 4 * (i % 2) + lo
+            nc.sync.dma_start(out=x_sb[i][:, lo : lo + n, :], in_=src[:, t0 : t0 + n, :])
 
         def tables():
             nc.vector.tensor_scalar_mul(out=u_t[:, 0:1], in0=one[:], scalar1=1.0 / (2.0 * math.pi))
@@ -245,23 +182,18 @@ def tile_multilatentattention_pb_t_kernel(tc, x, Wkva, Wkvb, out_0, out_1):
             )
             st[("pt", i)] = pt
 
-        def rope_add(i, eng):
+        def rope_add(i):
             pt = st[("pt", i)]
-            e = nc.gpsimd if eng == "G" else nc.vector
-            e.tensor_tensor(
+            nc.vector.tensor_tensor(
                 out=st[("kf", i)][:, 0, :, NOPE:].rearrange("p t (c r) -> p t c r", r=2),
                 in0=pt[:, :, 0, :, :].rearrange("p t r c -> p t c r"),
                 in1=pt[:, :, 1, :, :].rearrange("p t r c -> p t c r"),
                 op=ALU.add,
             )
 
-        def rope_rep(i, eng):
+        def rope_rep(i):
             kf = st[("kf", i)]
-            if eng == "G":
-                for h in range(1, H):
-                    copy("G", kf[:, h, :, NOPE:], kf[:, 0, :, NOPE:])
-            else:
-                copy(eng, kf[:, 1:H, :, NOPE:], kf[:, 0:1, :, NOPE:].to_broadcast([P, H - 1, 4, ROPE]))
+            nc.vector.tensor_copy(out=kf[:, 1:H, :, NOPE:], in_=kf[:, 0:1, :, NOPE:].to_broadcast([P, H - 1, 4, ROPE]))
 
         def latent_mm(i, j):
             ct = ps_mx.tile([P, 4, 128], F32, name="mx")
@@ -293,7 +225,7 @@ def tile_multilatentattention_pb_t_kernel(tc, x, Wkva, Wkvb, out_0, out_1):
                 in_=st[("cg", i)][:, 256 * pr : 256 * (pr + 1), :].rearrange("p w t -> p (w t)"),
             )
 
-        def kv_mm(i, j):
+        def kv_mm_out(i, j, eng):
             kv = ps_kv.tile([P, H, 2, 64], F32, name="kv")
             nc.tensor.matmul_mx(
                 out=kv[:].rearrange("p h s c -> p (h s c)"),
@@ -304,10 +236,6 @@ def tile_multilatentattention_pb_t_kernel(tc, x, Wkva, Wkvb, out_0, out_1):
                 start=True,
                 stop=True,
             )
-            st[("kv", i, j)] = kv
-
-        def kv_out(i, j, eng):
-            kv = st[("kv", i, j)]
             copy(eng, st[("kf", i)][:, :, j, 0:NOPE], kv[:, :, 0, :])
             copy(eng, st[("vv", i)][:, :, j, :], kv[:, :, 1, :])
 
@@ -323,63 +251,92 @@ def tile_multilatentattention_pb_t_kernel(tc, x, Wkva, Wkvb, out_0, out_1):
                 in_=st[("vv", i)][:, :, j_lo : j_lo + j_n, :],
             )
 
-        for t in PROGRAM:
-            k = t[0]
-            if k == "LD":
-                load(t[1])
-            elif k == "IOTA":
-                nc.gpsimd.iota(out=n_i[:], pattern=[[1, 8]], base=0, channel_multiplier=8)
-            elif k == "IDENT":
-                make_identity(nc, ident[:])
-            elif k == "SIN0":
-                nc.vector.memset(one[:], 1.0)
-                nc.scalar.activation(out=junk[:], in_=one[:], func=ACT.Sin)
-            elif k == "TABV":
-                tables()
-            elif k == "SIN2":
-                nc.scalar.activation(out=cs[:, :, 0, :], in_=t_a[:], func=ACT.Sin, scale=2.0 * math.pi)
-                nc.scalar.activation(out=cs[:, :, 1, :], in_=t_b[:], func=ACT.Sin, scale=-2.0 * math.pi)
-            elif k == "CSG":
-                nc.gpsimd.tensor_scalar(out=cs[:, :, 2, :], in0=cs[:, :, 1, :], scalar1=-1.0, scalar2=0.0, op0=ALU.mult, op1=ALU.add)
-                copy("G", cs[:, :, 3, :], cs[:, :, 0, :])
-            elif k == "RGA":
-                regroup_a(t[1], t[2], t[3], t[4])
-            elif k == "RGR":
-                regroup_r(t[1], t[2])
-            elif k == "QWA":
-                quant_w(t[1], 0, KVR)
-            elif k == "QWR":
-                quant_w(0, KVR, WA)
-                quant_w(1, KVR, WA)
-            elif k == "RGB":
-                regroup_b(t[1], t[2], t[3])
-            elif k == "QWB":
+        load_wa(0)
+        load_x(0, 0, 2)
+        load_wa(1)
+        load_x(0, 2, 2)
+        nc.sync.dma_start(out=wb_raw[:], in_=Wkvb.rearrange("(t p) n -> p t n", p=P))
+        for i in range(1, UNITS):
+            load_x(i, 0, 4)
+        nc.gpsimd.iota(out=n_i[:], pattern=[[1, 8]], base=0, channel_multiplier=8)
+        make_identity(nc, ident[:])
+        nc.vector.memset(one[:], 1.0)
+        nc.scalar.activation(out=junk[:], in_=one[:], func=ACT.Sin)
+        tables()
+        nc.scalar.activation(out=cs[:, :, 0, :], in_=t_a[:], func=ACT.Sin, scale=2.0 * math.pi)
+        nc.scalar.activation(out=cs[:, :, 1, :], in_=t_b[:], func=ACT.Sin, scale=-2.0 * math.pi)
+        regroup_a(0, "V", 0, KVR)
+        transposes(0, 0)
+        transposes(0, 1)
+        x_out(0, 0, "S")
+        x_out(0, 1, "S")
+        quant_w(0, 0, KVR)
+        regroup_a(1, "V", 0, 352)
+        regroup_a(1, "S", 352, KVR)
+        quant_x(0, 0)
+        quant_w(1, 0, KVR)
+        transposes(0, 2)
+        transposes(0, 3)
+        regroup_r(0, "S")
+        x_out(0, 2, "S")
+        x_out(0, 3, "S")
+        regroup_r(1, "S")
+        quant_x(0, 1)
+        quant_w(0, KVR, WA)
+        quant_w(1, KVR, WA)
+        nc.vector.tensor_scalar_mul(out=cs[:, :, 2, :], in0=cs[:, :, 1, :], scalar1=-1.0)
+        nc.vector.tensor_copy(out=cs[:, :, 3, :], in_=cs[:, :, 0, :])
+
+        for i in range(UNITS + 1):
+            nxt = i + 1 < UNITS
+            cur = i < UNITS
+            prv = i >= 1
+            last = i == UNITS
+            if prv:
+                quant_c(i - 1, 1)
+            if cur:
+                latent_mm(i, 0)
+                c_out(i, 0, "V")
+                latent_mm(i, 1)
+                c_out(i, 1, "S")
+            if prv:
+                rope_rep(i - 1)
+                kv_mm_out(i - 1, 2, "S")
+                if last:
+                    store(i - 1, 0, 3)
+                kv_mm_out(i - 1, 3, "V" if last else "S")
+                if last:
+                    store(i - 1, 3, 1)
+                else:
+                    store(i - 1, 0, 4)
+            if cur:
+                quant_c(i, 0)
+                rope_mm(i)
+                rope_mul(i)
+            if nxt:
+                transposes(i + 1, 0)
+                transposes(i + 1, 1)
+                transposes(i + 1, 2)
+                x_out(i + 1, 0, "S")
+                transposes(i + 1, 3)
+                x_out(i + 1, 1, "S")
+            if cur:
+                rope_add(i)
+            if i == 0:
+                regroup_b("V", 0, 256)
+                regroup_b("S", 256, 512)
                 nc.vector.quantize_mx(out=wb_c[:].bitcast(FP8X4), scales=wb_s[:], in_=wb_g[:].rearrange("p w t -> p (w t)"))
-            elif k == "T":
-                transposes(t[1], t[2])
-            elif k == "XO":
-                x_out(t[1], t[2], t[3])
-            elif k == "QX":
-                quant_x(t[1], t[2])
-            elif k == "R":
-                rope_mm(t[1])
-            elif k == "RM":
-                rope_mul(t[1])
-            elif k == "RA":
-                rope_add(t[1], t[2])
-            elif k == "RR":
-                rope_rep(t[1], t[2])
-            elif k == "S1":
-                latent_mm(t[1], t[2])
-            elif k == "CO":
-                c_out(t[1], t[2], t[3])
-            elif k == "QCP":
-                quant_c(t[1], t[2])
-            elif k == "S2":
-                kv_mm(t[1], t[2])
-            elif k == "KO":
-                kv_out(t[1], t[2], t[3])
-            elif k == "ST":
-                store(t[1], t[2], t[3])
-            else:
-                raise ValueError(k)
+            if nxt:
+                quant_x(i + 1, 0)
+                x_out(i + 1, 2, "S")
+                x_out(i + 1, 3, "S")
+            if cur:
+                latent_mm(i, 2)
+                c_out(i, 2, "V")
+                latent_mm(i, 3)
+                c_out(i, 3, "S")
+            if nxt:
+                quant_x(i + 1, 1)
+            if cur:
+                kv_mm_out(i, 0, "S")
+                kv_mm_out(i, 1, "S")

@@ -28,8 +28,8 @@ def tile_multilatentattention_pb_t_kernel(tc, x, Wkva, Wkvb, out_0, out_1):
         const = ctx.enter_context(tc.tile_pool(name="const", bufs=1))
         work = ctx.enter_context(tc.tile_pool(name="work", bufs=2))
         outp = ctx.enter_context(tc.tile_pool(name="outp", bufs=3))
-        ps_xt = ctx.enter_context(tc.psum_pool(name="ps_xt", bufs=3))
-        ps_mx = ctx.enter_context(tc.psum_pool(name="ps_mx", bufs=3))
+        ps_xt = ctx.enter_context(tc.psum_pool(name="ps_xt", bufs=4))
+        ps_mx = ctx.enter_context(tc.psum_pool(name="ps_mx", bufs=2))
         ps_kv = ctx.enter_context(tc.psum_pool(name="ps_kv", bufs=2))
 
         wa_raw = const.tile([P, 2, 4, WA], BF16)
@@ -302,13 +302,8 @@ def tile_multilatentattention_pb_t_kernel(tc, x, Wkva, Wkvb, out_0, out_1):
             if prv:
                 rope_rep(i - 1)
                 kv_mm_out(i - 1, 2, "S")
-                if last:
-                    store(i - 1, 0, 3)
                 kv_mm_out(i - 1, 3, "V" if last else "S")
-                if last:
-                    store(i - 1, 3, 1)
-                else:
-                    store(i - 1, 0, 4)
+                store(i - 1, 0, 4)
             if cur:
                 quant_c(i, 0)
                 rope_mm(i)

@@ -28,8 +28,8 @@ def tile_multilatentattention_pb_t_kernel(tc, x, Wkva, Wkvb, out_0, out_1):
         const = ctx.enter_context(tc.tile_pool(name="const", bufs=1))
         work = ctx.enter_context(tc.tile_pool(name="work", bufs=2))
         outp = ctx.enter_context(tc.tile_pool(name="outp", bufs=3))
-        ps_xt = ctx.enter_context(tc.psum_pool(name="ps_xt", bufs=4))
-        ps_mx = ctx.enter_context(tc.psum_pool(name="ps_mx", bufs=2))
+        ps_xt = ctx.enter_context(tc.psum_pool(name="ps_xt", bufs=2))
+        ps_mx = ctx.enter_context(tc.psum_pool(name="ps_mx", bufs=4))
         ps_kv = ctx.enter_context(tc.psum_pool(name="ps_kv", bufs=2))
 
         wa_raw = const.tile([P, 2, 4, WA], BF16)
@@ -112,11 +112,11 @@ def tile_multilatentattention_pb_t_kernel(tc, x, Wkva, Wkvb, out_0, out_1):
                 in_=wa_g[:, g, lo:hi, :].rearrange("p w t -> p (w t)"),
             )
 
-        def regroup_b(eng, lo, hi):
+        def regroup_b(eng, s):
             copy(
                 eng,
-                wb_g[:, lo:hi, :].rearrange("p (c i) t -> p c t i", i=4),
-                wb_raw[:, :, lo:hi].rearrange("p t (c i) -> p c t i", i=4),
+                wb_g[:, 256 * s : 256 * (s + 1), :].rearrange("p (h c) t -> p h c t", h=H),
+                wb_raw[:].rearrange("p t (h s c) -> p s h c t", h=H, s=2)[:, s],
             )
 
         def transposes(i, q):
@@ -225,19 +225,24 @@ def tile_multilatentattention_pb_t_kernel(tc, x, Wkva, Wkvb, out_0, out_1):
                 in_=st[("cg", i)][:, 256 * pr : 256 * (pr + 1), :].rearrange("p w t -> p (w t)"),
             )
 
-        def kv_mm_out(i, j, eng):
-            kv = ps_kv.tile([P, H, 2, 64], F32, name="kv")
-            nc.tensor.matmul_mx(
-                out=kv[:].rearrange("p h s c -> p (h s c)"),
-                lhsT=st[("cc", i)][:, 128 * j : 128 * (j + 1)].bitcast(FP8X4),
-                lhsT_scale=st[("cs", i)][:, 128 * j : 128 * (j + 1)],
-                rhs=wb_c[:].bitcast(FP8X4),
-                rhs_scale=wb_s[:],
-                start=True,
-                stop=True,
-            )
-            copy(eng, st[("kf", i)][:, :, j, 0:NOPE], kv[:, :, 0, :])
-            copy(eng, st[("vv", i)][:, :, j, :], kv[:, :, 1, :])
+        def kv_mm_out(i, pr, eng_k, eng_v):
+            banks = []
+            for s in range(2):
+                banks.append(ps_kv.tile([P, 2, H, 64], F32, name="kv"))
+            for jj in range(2):
+                j = 2 * pr + jj
+                for s in range(2):
+                    nc.tensor.matmul_mx(
+                        out=banks[s][:, jj, :, :].rearrange("p h c -> p (h c)"),
+                        lhsT=st[("cc", i)][:, 128 * j : 128 * (j + 1)].bitcast(FP8X4),
+                        lhsT_scale=st[("cs", i)][:, 128 * j : 128 * (j + 1)],
+                        rhs=wb_c[:, 256 * s : 256 * (s + 1)].bitcast(FP8X4),
+                        rhs_scale=wb_s[:, 256 * s : 256 * (s + 1)],
+                        start=True,
+                        stop=True,
+                    )
+            copy(eng_k, st[("kf", i)][:, :, 2 * pr : 2 * pr + 2, 0:NOPE].rearrange("p h j c -> p j h c"), banks[0][:])
+            copy(eng_v, st[("vv", i)][:, :, 2 * pr : 2 * pr + 2, :].rearrange("p h j c -> p j h c"), banks[1][:])
 
         def store(i, j_lo, j_n):
             b = i // 2
@@ -299,39 +304,45 @@ def tile_multilatentattention_pb_t_kernel(tc, x, Wkva, Wkvb, out_0, out_1):
                 c_out(i, 0, "V")
                 latent_mm(i, 1)
                 c_out(i, 1, "S")
-            if prv:
-                rope_rep(i - 1)
-                kv_mm_out(i - 1, 2, "S")
-                kv_mm_out(i - 1, 3, "V" if last else "S")
-                store(i - 1, 0, 4)
-            if cur:
-                quant_c(i, 0)
-                rope_mm(i)
-                rope_mul(i)
             if nxt:
                 transposes(i + 1, 0)
                 transposes(i + 1, 1)
-                transposes(i + 1, 2)
                 x_out(i + 1, 0, "S")
-                transposes(i + 1, 3)
                 x_out(i + 1, 1, "S")
+            if prv:
+                if not last:
+                    rope_rep(i - 1)
+                kv_mm_out(i - 1, 1, "S", "V" if last else "S")
+                if last:
+                    store(i - 1, 2, 2)
+                else:
+                    store(i - 1, 0, 4)
             if cur:
-                rope_add(i)
+                quant_c(i, 0)
             if i == 0:
-                regroup_b("V", 0, 256)
-                regroup_b("S", 256, 512)
+                regroup_b("V", 0)
+                regroup_b("S", 1)
                 nc.vector.quantize_mx(out=wb_c[:].bitcast(FP8X4), scales=wb_s[:], in_=wb_g[:].rearrange("p w t -> p (w t)"))
             if nxt:
                 quant_x(i + 1, 0)
+            if cur:
+                rope_mm(i)
+                rope_mul(i)
+                latent_mm(i, 2)
+                c_out(i, 2, "V")
+                rope_add(i)
+            if nxt:
+                transposes(i + 1, 2)
+                transposes(i + 1, 3)
                 x_out(i + 1, 2, "S")
                 x_out(i + 1, 3, "S")
             if cur:
-                latent_mm(i, 2)
-                c_out(i, 2, "V")
                 latent_mm(i, 3)
                 c_out(i, 3, "S")
+                if i == UNITS - 1:
+                    rope_rep(i)
+                kv_mm_out(i, 0, "S", "S")
+                if i == UNITS - 1:
+                    store(i, 0, 2)
             if nxt:
                 quant_x(i + 1, 1)
-            if cur:
-                kv_mm_out(i, 0, "S")
-                kv_mm_out(i, 1, "S")

@@ -193,7 +193,10 @@ def tile_multilatentattention_pb_t_kernel(tc, x, Wkva, Wkvb, out_0, out_1):
 
         def rope_rep(i):
             kf = st[("kf", i)]
-            nc.vector.tensor_copy(out=kf[:, 1:H, :, NOPE:], in_=kf[:, 0:1, :, NOPE:].to_broadcast([P, H - 1, 4, ROPE]))
+            nc.vector.tensor_copy(
+                out=kf[:, 1:H, :, NOPE:].rearrange("p h t c -> p t h c"),
+                in_=kf[:, 0, :, NOPE:].unsqueeze(2).to_broadcast([P, 4, H - 1, ROPE]),
+            )
 
         def latent_mm(i, j):
             ct = ps_mx.tile([P, 4, 128], F32, name="mx")
@@ -270,6 +273,8 @@ def tile_multilatentattention_pb_t_kernel(tc, x, Wkva, Wkvb, out_0, out_1):
         tables()
         nc.scalar.activation(out=cs[:, :, 0, :], in_=t_a[:], func=ACT.Sin, scale=2.0 * math.pi)
         nc.scalar.activation(out=cs[:, :, 1, :], in_=t_b[:], func=ACT.Sin, scale=-2.0 * math.pi)
+        nc.scalar.activation(out=cs[:, :, 2, :], in_=t_b[:], func=ACT.Sin, scale=2.0 * math.pi)
+        nc.scalar.activation(out=cs[:, :, 3, :], in_=t_a[:], func=ACT.Sin, scale=2.0 * math.pi)
         regroup_a(0, "V", 0, KVR)
         transposes(0, 0)
         transposes(0, 1)
@@ -289,8 +294,6 @@ def tile_multilatentattention_pb_t_kernel(tc, x, Wkva, Wkvb, out_0, out_1):
         quant_x(0, 1)
         quant_w(0, KVR, WA)
         quant_w(1, KVR, WA)
-        nc.vector.tensor_scalar_mul(out=cs[:, :, 2, :], in0=cs[:, :, 1, :], scalar1=-1.0)
-        nc.vector.tensor_copy(out=cs[:, :, 3, :], in_=cs[:, :, 0, :])
 
         for i in range(UNITS + 1):
             nxt = i + 1 < UNITS

@@ -273,8 +273,6 @@ def tile_multilatentattention_pb_t_kernel(tc, x, Wkva, Wkvb, out_0, out_1):
         tables()
         nc.scalar.activation(out=cs[:, :, 0, :], in_=t_a[:], func=ACT.Sin, scale=2.0 * math.pi)
         nc.scalar.activation(out=cs[:, :, 1, :], in_=t_b[:], func=ACT.Sin, scale=-2.0 * math.pi)
-        nc.scalar.activation(out=cs[:, :, 2, :], in_=t_b[:], func=ACT.Sin, scale=2.0 * math.pi)
-        nc.scalar.activation(out=cs[:, :, 3, :], in_=t_a[:], func=ACT.Sin, scale=2.0 * math.pi)
         regroup_a(0, "V", 0, KVR)
         transposes(0, 0)
         transposes(0, 1)
@@ -294,6 +292,8 @@ def tile_multilatentattention_pb_t_kernel(tc, x, Wkva, Wkvb, out_0, out_1):
         quant_x(0, 1)
         quant_w(0, KVR, WA)
         quant_w(1, KVR, WA)
+        nc.vector.tensor_scalar_mul(out=cs[:, :, 2, :], in0=cs[:, :, 1, :], scalar1=-1.0)
+        nc.vector.tensor_copy(out=cs[:, :, 3, :], in_=cs[:, :, 0, :])
 
         for i in range(UNITS + 1):
             nxt = i + 1 < UNITS

@@ -24,7 +24,6 @@ FLOPS = 2 * B * N * E * WA + 2 * B * N * KVR * H * (NOPE + VDIM)
 def tile_multilatentattention_pb_t_kernel(tc, x, Wkva, Wkvb, out_0, out_1):
     nc = tc.nc
     with ExitStack() as ctx:
-        ctx.enter_context(tc.manual_schedule())
         const = ctx.enter_context(tc.tile_pool(name="const", bufs=1))
         work = ctx.enter_context(tc.tile_pool(name="work", bufs=2))
         outp = ctx.enter_context(tc.tile_pool(name="outp", bufs=3))

import math
from contextlib import ExitStack

import concourse.mybir as mybir
from concourse.masks import make_identity

F32 = mybir.dt.float32
BF16 = mybir.dt.bfloat16
U32 = mybir.dt.uint32
U8 = mybir.dt.uint8
I32 = mybir.dt.int32
FP8X4 = mybir.dt.float8_e4m3fn_x4
ALU = mybir.AluOpType
ACT = mybir.ActivationFunctionType

P = 128
B, N, E, H, NOPE, VDIM, ROPE, KVR = 4, 1024, 1024, 4, 64, 64, 128, 512
BASE = 10000.0
WA = KVR + ROPE
UNITS = 8
FLOPS = 2 * B * N * E * WA + 2 * B * N * KVR * H * (NOPE + VDIM)


def tile_multilatentattention_pb_t_kernel(tc, x, Wkva, Wkvb, out_0, out_1):
    nc = tc.nc
    with ExitStack() as ctx:
        const = ctx.enter_context(tc.tile_pool(name="const", bufs=1))
        work = ctx.enter_context(tc.tile_pool(name="work", bufs=2))
        outp = ctx.enter_context(tc.tile_pool(name="outp", bufs=3))
        ps_xt = ctx.enter_context(tc.psum_pool(name="ps_xt", bufs=2))
        ps_mx = ctx.enter_context(tc.psum_pool(name="ps_mx", bufs=4))
        ps_kv = ctx.enter_context(tc.psum_pool(name="ps_kv", bufs=2))

        wa_raw = const.tile([P, 2, 4, WA], BF16)
        wb_raw = const.tile([P, 4, 512], BF16)
        x_sb = []
        for i in range(UNITS):
            x_sb.append(const.tile([P, 4, E], BF16, name="x_sb%d" % i))
        ident = const.tile([P, P], F32)
        n_i = const.tile([P, 8], I32)
        n_f = const.tile([P, 8], F32)
        one = const.tile([P, 1], F32)
        junk = const.tile([P, 1], F32)
        u_t = const.tile([P, 64], F32)
        t_a = const.tile([P, 8, 64], F32)
        t_b = const.tile([P, 8, 64], F32)
        t_k = const.tile([P, 8, 64], I32)
        cs = const.tile([P, 8, 4, 64], F32)
        wa_g = const.tile([P, 2, WA, 4], BF16, align_bytes=64)
        wa_c = const.tile([P, 2, WA], U32, align_bytes=64)
        wa_s = const.tile([P, 2, WA], U8, align_bytes=64)
        wb_g = const.tile([P, 512, 4], BF16, align_bytes=64)
        wb_c = const.tile([P, 512], U32, align_bytes=64)
        wb_s = const.tile([P, 512], U8, align_bytes=64)
        st = {}

        def copy(eng, out, in_):
            if eng == "S":
                nc.scalar.copy(out=out, in_=in_)
            else:
                nc.vector.tensor_copy(out=out, in_=in_)

        def load_wa(g):
            nc.sync.dma_start(
                out=wa_raw[:, g, :, :].rearrange("p (u e) c -> p u (e c)", e=2),
                in_=Wkva[512 * g : 512 * (g + 1), :].rearrange("(u q e) c -> q u (e c)", u=2, e=2),
            )

        def load_x(i, lo, n):
            src = x[i // 2].rearrange("(p t) k -> p t k", t=8)
            t0 = 4 * (i % 2) + lo
            nc.sync.dma_start(out=x_sb[i][:, lo : lo + n, :], in_=src[:, t0 : t0 + n, :])

        def tables():
            nc.vector.tensor_scalar_mul(out=u_t[:, 0:1], in0=one[:], scalar1=1.0 / (2.0 * math.pi))
            s = 1
            while s < 64:
                nc.vector.tensor_scalar_mul(out=u_t[:, s : 2 * s], in0=u_t[:, 0:s], scalar1=BASE ** (-2.0 * s / ROPE))
                s *= 2
            nc.vector.tensor_copy(out=n_f[:], in_=n_i[:])
            nc.vector.tensor_tensor(
                out=t_a[:],
                in0=n_f[:].unsqueeze(2).to_broadcast([P, 8, 64]),
                in1=u_t[:].unsqueeze(1).to_broadcast([P, 8, 64]),
                op=ALU.mult,
            )
            nc.vector.tensor_copy(out=t_k[:], in_=t_a[:])
            nc.vector.tensor_tensor(out=t_a[:], in0=t_a[:], in1=t_k[:], op=ALU.subtract)
            nc.vector.scalar_tensor_tensor(out=t_b[:], in0=t_a[:], scalar=0.5, in1=t_a[:], op0=ALU.is_gt, op1=ALU.subtract)
            nc.vector.scalar_tensor_tensor(out=t_a[:], in0=t_b[:], scalar=-1.0, in1=t_b[:], op0=ALU.mult, op1=ALU.min)
            nc.vector.tensor_scalar_add(out=t_a[:], in0=t_a[:], scalar1=0.25)

        def regroup_a(g, eng, lo, hi):
            copy(
                eng,
                wa_g[:, g, lo:hi, :].rearrange("p (c i) t -> p c t i", i=4),
                wa_raw[:, g, :, lo:hi].rearrange("p t (c i) -> p c t i", i=4),
            )

        def regroup_r(g, eng):
            copy(
                eng,
                wa_g[:, g, KVR:WA, :].rearrange("p (h i) t -> p h i t", h=2),
                wa_raw[:, g, :, KVR:WA].rearrange("p t (i h) -> p h i t", h=2),
            )

        def quant_w(g, lo, hi):
            nc.vector.quantize_mx(
                out=wa_c[:, g, lo:hi].bitcast(FP8X4),
                scales=wa_s[:, g, lo:hi],
                in_=wa_g[:, g, lo:hi, :].rearrange("p w t -> p (w t)"),
            )

        def regroup_b(eng, s):
            copy(
                eng,
                wb_g[:, 256 * s : 256 * (s + 1), :].rearrange("p (h c) t -> p h c t", h=H),
                wb_raw[:].rearrange("p t (h s c) -> p s h c t", h=H, s=2)[:, s],
            )

        def transposes(i, q):
            pr, g = q // 2, q % 2
            xt = ps_xt.tile([P, 2, 256], F32, name="xt")
            for u in range(2):
                for jj in range(2):
                    c0 = 256 * g + 128 * u
                    nc.tensor.transpose(
                        xt[:, u, 128 * jj : 128 * (jj + 1)],
                        x_sb[i][:, 2 * pr + jj, :].bitcast(F32)[:, c0 : c0 + 128],
                        ident[:],
                    )
            st[("xt", i, q)] = xt
            if q == 0:
                st[("xg", i)] = work.tile([P, 2048], F32, name="xg", align_bytes=64)
                st[("xc", i)] = work.tile([P, 1024], U32, name="xc", align_bytes=64)
                st[("xs", i)] = work.tile([P, 1024], U8, name="xs", align_bytes=64)

        def x_out(i, q, eng):
            copy(
                eng,
                st[("xg", i)][:, 512 * q : 512 * (q + 1)].rearrange("p (r u) -> p r u", u=2),
                st[("xt", i, q)][:].rearrange("p u r -> p r u"),
            )

        def quant_x(i, pr):
            nc.vector.quantize_mx(
                out=st[("xc", i)][:, 512 * pr : 512 * (pr + 1)].bitcast(FP8X4),
                scales=st[("xs", i)][:, 512 * pr : 512 * (pr + 1)],
                in_=st[("xg", i)][:, 1024 * pr : 1024 * (pr + 1)].bitcast(BF16),
            )

        def x_cols(j, g):
            c0 = ((j // 2) * 2 + g) * 256 + (j % 2) * 128
            return slice(c0, c0 + 128)

        def rope_mm(i):
            kp = ps_mx.tile([P, 4, 128], F32, name="mx")
            for j in range(4):
                for g in range(2):
                    nc.tensor.matmul_mx(
                        out=kp[:, j, :],
                        lhsT=st[("xc", i)][:, x_cols(j, g)].bitcast(FP8X4),
                        lhsT_scale=st[("xs", i)][:, x_cols(j, g)],
                        rhs=wa_c[:, g, KVR:WA].bitcast(FP8X4),
                        rhs_scale=wa_s[:, g, KVR:WA],
                        start=(g == 0),
                        stop=(g == 1),
                    )
            st[("kp", i)] = kp
            st[("kf", i)] = outp.tile([P, H, 4, NOPE + ROPE], F32, name="kf")
            st[("vv", i)] = outp.tile([P, H, 4, VDIM], F32, name="vv")

        def rope_mul(i):
            pt = work.tile([P, 4, 2, 2, 64], F32, name="pt")
            t0 = 4 * (i % 2)
            nc.vector.tensor_tensor(
                out=pt[:].rearrange("p t h r c -> p (t h) r c"),
                in0=st[("kp", i)][:].rearrange("p t (h c) -> p (t h) c", h=2).unsqueeze(2).to_broadcast([P, 8, 2, 64]),
                in1=cs[:, t0 : t0 + 4, :, :].rearrange("p t (h r) c -> p (t h) r c", h=2),
                op=ALU.mult,
            )
            st[("pt", i)] = pt

        def rope_add(i):
            pt = st[("pt", i)]
            nc.vector.tensor_tensor(
                out=st[("kf", i)][:, 0, :, NOPE:].rearrange("p t (c r) -> p t c r", r=2),
                in0=pt[:, :, 0, :, :].rearrange("p t r c -> p t c r"),
                in1=pt[:, :, 1, :, :].rearrange("p t r c -> p t c r"),
                op=ALU.add,
            )

        def rope_rep(i):
            kf = st[("kf", i)]
            nc.vector.tensor_copy(
                out=kf[:, 1:H, :, NOPE:].rearrange("p h t c -> p t h c"),
                in_=kf[:, 0, :, NOPE:].unsqueeze(2).to_broadcast([P, 4, H - 1, ROPE]),
            )

        def latent_mm(i, j):
            ct = ps_mx.tile([P, 4, 128], F32, name="mx")
            for m in range(4):
                for g in range(2):
                    nc.tensor.matmul_mx(
                        out=ct[:, m, :],
                        lhsT=wa_c[:, g, 128 * m : 128 * (m + 1)].bitcast(FP8X4),
                        lhsT_scale=wa_s[:, g, 128 * m : 128 * (m + 1)],
                        rhs=st[("xc", i)][:, x_cols(j, g)].bitcast(FP8X4),
                        rhs_scale=st[("xs", i)][:, x_cols(j, g)],
                        start=(g == 0),
                        stop=(g == 1),
                    )
            st[("ct", i, j)] = ct
            if j == 0:
                st[("cg", i)] = work.tile([P, 512, 4], BF16, name="cg", align_bytes=64)

        def c_out(i, j, eng):
            copy(eng, st[("cg", i)][:, 128 * j : 128 * (j + 1), :], st[("ct", i, j)][:].rearrange("p m r -> p r m"))

        def quant_c(i, pr):
            if pr == 0:
                st[("cc", i)] = work.tile([P, 512], U32, name="cc", align_bytes=64)
                st[("cs", i)] = work.tile([P, 512], U8, name="csc", align_bytes=64)
            nc.vector.quantize_mx(
                out=st[("cc", i)][:, 256 * pr : 256 * (pr + 1)].bitcast(FP8X4),
                scales=st[("cs", i)][:, 256 * pr : 256 * (pr + 1)],
                in_=st[("cg", i)][:, 256 * pr : 256 * (pr + 1), :].rearrange("p w t -> p (w t)"),
            )

        def kv_mm_out(i, pr, eng_k, eng_v):
            banks = []
            for s in range(2):
                banks.append(ps_kv.tile([P, 2, H, 64], F32, name="kv"))
            for jj in range(2):
                j = 2 * pr + jj
                for s in range(2):
                    nc.tensor.matmul_mx(
                        out=banks[s][:, jj, :, :].rearrange("p h c -> p (h c)"),
                        lhsT=st[("cc", i)][:, 128 * j : 128 * (j + 1)].bitcast(FP8X4),
                        lhsT_scale=st[("cs", i)][:, 128 * j : 128 * (j + 1)],
                        rhs=wb_c[:, 256 * s : 256 * (s + 1)].bitcast(FP8X4),
                        rhs_scale=wb_s[:, 256 * s : 256 * (s + 1)],
                        start=True,
                        stop=True,
                    )
            copy(eng_k, st[("kf", i)][:, :, 2 * pr : 2 * pr + 2, 0:NOPE].rearrange("p h j c -> p j h c"), banks[0][:])
            copy(eng_v, st[("vv", i)][:, :, 2 * pr : 2 * pr + 2, :].rearrange("p h j c -> p j h c"), banks[1][:])

        def store(i, j_lo, j_n):
            b = i // 2
            t0 = 4 * (i % 2) + j_lo
            nc.sync.dma_start(
                out=out_0[b].rearrange("h (p t) f -> p h t f", t=8)[:, :, t0 : t0 + j_n, :],
                in_=st[("kf", i)][:, :, j_lo : j_lo + j_n, :],
            )
            nc.sync.dma_start(
                out=out_1[b].rearrange("h (p t) f -> p h t f", t=8)[:, :, t0 : t0 + j_n, :],
                in_=st[("vv", i)][:, :, j_lo : j_lo + j_n, :],
            )

        load_wa(0)
        load_x(0, 0, 2)
        load_wa(1)
        load_x(0, 2, 2)
        nc.sync.dma_start(out=wb_raw[:], in_=Wkvb.rearrange("(t p) n -> p t n", p=P))
        for i in range(1, UNITS):
            load_x(i, 0, 4)
        nc.gpsimd.iota(out=n_i[:], pattern=[[1, 8]], base=0, channel_multiplier=8)
        make_identity(nc, ident[:])
        nc.vector.memset(one[:], 1.0)
        nc.scalar.activation(out=junk[:], in_=one[:], func=ACT.Sin)
        tables()
        nc.scalar.activation(out=cs[:, :, 0, :], in_=t_a[:], func=ACT.Sin, scale=2.0 * math.pi)
        nc.scalar.activation(out=cs[:, :, 1, :], in_=t_b[:], func=ACT.Sin, scale=-2.0 * math.pi)
        regroup_a(0, "V", 0, KVR)
        transposes(0, 0)
        transposes(0, 1)
        x_out(0, 0, "S")
        x_out(0, 1, "S")
        quant_w(0, 0, KVR)
        regroup_a(1, "V", 0, 352)
        regroup_a(1, "S", 352, KVR)
        quant_x(0, 0)
        quant_w(1, 0, KVR)
        transposes(0, 2)
        transposes(0, 3)
        regroup_r(0, "S")
        x_out(0, 2, "S")
        x_out(0, 3, "S")
        regroup_r(1, "S")
        quant_x(0, 1)
        quant_w(0, KVR, WA)
        quant_w(1, KVR, WA)
        nc.vector.tensor_scalar_mul(out=cs[:, :, 2, :], in0=cs[:, :, 1, :], scalar1=-1.0)
        nc.vector.tensor_copy(out=cs[:, :, 3, :], in_=cs[:, :, 0, :])

        for i in range(UNITS + 1):
            nxt = i + 1 < UNITS
            cur = i < UNITS
            prv = i >= 1
            last = i == UNITS
            if prv:
                quant_c(i - 1, 1)
            if cur:
                latent_mm(i, 0)
                c_out(i, 0, "V")
                latent_mm(i, 1)
                c_out(i, 1, "S")
            if nxt:
                transposes(i + 1, 0)
                transposes(i + 1, 1)
                x_out(i + 1, 0, "S")
                x_out(i + 1, 1, "S")
            if prv:
                if not last:
                    rope_rep(i - 1)
                kv_mm_out(i - 1, 1, "S", "V" if last else "S")
                if last:
                    store(i - 1, 2, 2)
                else:
                    store(i - 1, 0, 4)
            if cur:
                quant_c(i, 0)
            if i == 0:
                regroup_b("V", 0)
                regroup_b("S", 1)
                nc.vector.quantize_mx(out=wb_c[:].bitcast(FP8X4), scales=wb_s[:], in_=wb_g[:].rearrange("p w t -> p (w t)"))
            if nxt:
                quant_x(i + 1, 0)
            if cur:
                rope_mm(i)
                rope_mul(i)
                latent_mm(i, 2)
                c_out(i, 2, "V")
                rope_add(i)
            if nxt:
                transposes(i + 1, 2)
                transposes(i + 1, 3)
                x_out(i + 1, 2, "S")
                x_out(i + 1, 3, "S")
            if cur:
                latent_mm(i, 3)
                c_out(i, 3, "S")
                if i == UNITS - 1:
                    rope_rep(i)
                kv_mm_out(i, 0, "S", "S")
                if i == UNITS - 1:
                    store(i, 0, 2)
            if nxt:
                quant_x(i + 1, 1)
